import numpy as np
import ml_dtypes


def mxq(x, axis, fmt="e4m3"):
    dtype, down = {"e4m3": (ml_dtypes.float8_e4m3fn, 7), "e5m2": (ml_dtypes.float8_e5m2, 14)}[fmt]
    v = np.moveaxis(np.asarray(x, np.float32).astype(ml_dtypes.bfloat16).astype(np.float64), axis, -1)
    blocks = v.reshape(v.shape[:-1] + (-1, 32))
    amax = np.abs(blocks).max(-1, keepdims=True)
    byte = np.maximum(np.where(amax > 0, np.frexp(amax)[1] - 1 + 127, 0) - down, 1)
    scale = np.exp2(byte - 127.0)
    codes = (blocks / scale).astype(np.float32).astype(dtype).astype(np.float64)
    return np.moveaxis((codes * scale).reshape(v.shape), -1, axis)


WIDE = False


def mx_kscale(k):
    if not WIDE:
        return np.ones(k)
    levels = np.array([10, -10, 5, -5, 0])
    if k % 512:
        return np.exp2(np.random.permutation(np.resize(levels, k // 32))).repeat(32)
    a = np.empty((k // 512, 16))
    for p in range(k // 512):
        a[p, :8] = np.random.permutation(np.resize(levels, 8))
        for g in range(8):
            far = levels[np.abs(levels - a[p, g]) >= 10]
            a[p, g + 8] = far[np.random.randint(len(far))]
    return np.exp2(a.ravel()).repeat(32)


BF16 = ml_dtypes.bfloat16


def bf(x):
    return np.asarray(x, np.float32).astype(BF16)


def f64(x):
    return np.asarray(x).astype(np.float64)


B, C, H, W, P, DIM = 8, 8, 128, 128, 16, 768
SHIFT = P // 2
WD = 5 * C * P * P // 4
N = (H // P) * (W // P)
EPS = 1e-5
XS = 0.015


def patch_shift(x, shift):
    xp = np.pad(x, ((0, 0), (0, 0), (shift, shift), (shift, shift)))
    s2 = 2 * shift
    return np.concatenate([x, xp[:, :, :-s2, :-s2], xp[:, :, :-s2, s2:], xp[:, :, s2:, :-s2], xp[:, :, s2:, s2:]], axis=1)


def haar_detail_mean(x):
    b_, c_, h, w = x.shape
    r = x.reshape(b_, c_, h // 2, 2, w // 2, 2)
    return (3.0 * r[:, :, :, 0, :, 0] - r[:, :, :, 0, :, 1] - r[:, :, :, 1, :, 0] - r[:, :, :, 1, :, 1]) / 6.0


def patchify(x, p):
    b_, c_, hh, ww = x.shape
    h, w = hh // p, ww // p
    return x.reshape(b_, c_, h, p, w, p).transpose(0, 2, 4, 3, 5, 1).reshape(b_, h * w, p * p * c_)


def layernorm(u, g, b):
    m = u.mean(-1, keepdims=True)
    v = np.square(u - m).mean(-1, keepdims=True)
    return (u - m) / np.sqrt(v + EPS) * g + b


def setup_inputs():
    s = mx_kscale(WD)
    return {"x": bf(np.random.standard_normal((B, C, H, W)) * XS),
            "ln2_g": bf((1.0 + 0.1 * np.random.standard_normal(WD)) * s),
            "ln2_b": bf(0.1 * np.random.standard_normal(WD) * s),
            "w2": bf(np.random.standard_normal((WD, DIM)) / np.sqrt(WD) / s[:, None]),
            "b2": bf(0.3 * np.random.standard_normal(DIM)),
            "tok": bf(np.random.standard_normal((B, N, DIM)))}


def reference(x, ln2_g, ln2_b, w2, b2, tok):
    waves = haar_detail_mean(patch_shift(f64(x), SHIFT))
    z = layernorm(patchify(waves, P // 2), f64(ln2_g), f64(ln2_b))
    wtok = (mxq(z, 2, "e4m3") @ mxq(f64(w2), 0, "e4m3")) + f64(b2)
    return f64(tok) + wtok

@@ -1,0 +1,437 @@
+from contextlib import ExitStack
+
+import concourse.mybir as mybir
+from concourse.masks import make_identity
+
+F32 = mybir.dt.float32
+BF16 = mybir.dt.bfloat16
+U32 = mybir.dt.uint32
+U8 = mybir.dt.uint8
+FP8X4 = mybir.dt.float8_e4m3fn_x4
+ALU = mybir.AluOpType
+ACT = mybir.ActivationFunctionType
+AX = mybir.AxisListType
+
+P = 128
+BATCH = 8
+CH = 8
+BANDS = 16
+BAND_ROWS = 4
+DETAIL_W = 64
+PAD = 4
+PADDED_W = DETAIL_W + 2 * PAD
+ROW_LEN = PADDED_W * CH
+BAND_LEN = BAND_ROWS * ROW_LEN
+GRID = 8
+PATCH = 8
+VIEWS = 5
+HALF_K = BAND_ROWS * PATCH * VIEWS * CH
+K = 2 * HALF_K
+DIM = 768
+TOKENS = BATCH * GRID * GRID
+PACK = 4
+PASS_K = P * PACK
+WINDOWS = (0, 512, 768)
+PASSES = 2 * len(WINDOWS)
+SLOTS = PASSES * PACK
+HALF_SLOTS = SLOTS // 2
+J_GROUP = 4
+J_GROUPS = GRID // J_GROUP
+GROUP_TOKENS = TOKENS // J_GROUPS
+N_WIDE = 512
+WIDE = slice(0, N_WIDE)
+REST = slice(N_WIDE, DIM)
+PASS_ORDER = [3 * h + w for w in range(3) for h in range(2)]
+STEPS = J_GROUPS * HALF_SLOTS
+TURN_BANKS = 4
+AHEAD = TURN_BANKS - 1
+LAG = 6
+LAST_W_STEP = 6
+EARLY_W = 4
+HAAR_SCALE = 6.0
+EPS = 1e-5 * HAAR_SCALE * HAAR_SCALE
+
+FLOPS = 2 * TOKENS * K * DIM
+
+
+def tile_shiftedpatchtokenization_pb_kernel(tc, x, ln2_g, ln2_b, w2, b2, tok, out):
+    nc = tc.nc
+    with ExitStack() as ctx:
+        keep = ctx.enter_context(tc.tile_pool(name="keep", bufs=1))
+        w_raw_pool = ctx.enter_context(tc.tile_pool(name="w_raw", bufs=EARLY_W))
+        w_grp_pool = ctx.enter_context(tc.tile_pool(name="w_grp", bufs=3))
+        z_grp_pool = ctx.enter_context(tc.tile_pool(name="z_grp", bufs=3))
+        turn_psum = ctx.enter_context(tc.psum_pool(name="turn_psum", bufs=TURN_BANKS))
+        acc_psum = ctx.enter_context(tc.psum_pool(name="acc_psum", bufs=1))
+        ctx.enter_context(tc.manual_schedule())
+
+        image = keep.tile([P, CH, 8 * 128], BF16, tag="image")
+        w_raws = {}
+        w_codes = keep.tile([P, PASSES, DIM], U32, align_bytes=64)
+        w_scales = keep.tile([P, PASSES, DIM], U8, align_bytes=64)
+        z_codes = keep.tile([P, PASSES, TOKENS], U32, align_bytes=64)
+        z_scales = keep.tile([P, PASSES, TOKENS], U8, align_bytes=64)
+        tok_in = keep.tile([P, 4, DIM], BF16)
+        tok_bias = keep.tile([P, 4, DIM], F32)
+        detail = keep.tile([P, BAND_ROWS, PADDED_W, CH], F32)
+        detail_up = keep.tile([P, BAND_ROWS, PADDED_W, CH], F32)
+        detail_dn = keep.tile([P, BAND_ROWS, PADDED_W, CH], F32)
+        scratch = out.rearrange("b n d -> (b n d)")[0 : (P + 2 * BATCH) * BAND_LEN].rearrange("(q f) -> q f", f=BAND_LEN)
+
+        def token_rows(dram, m):
+            jq, bh = divmod(m, 2)
+            rows = dram[4 * bh : 4 * bh + 4, :, :]
+            return rows.rearrange("b (i q j) d -> q (b i) j d", q=J_GROUPS, j=J_GROUP)[jq]
+
+        def load_image(c):
+            nc.sync.dma_start(out=image[:, c, :], in_=x[:, c, :, :].rearrange("b (a r) w -> a b (r w)", a=BANDS))
+
+        def load_w(g):
+            h, w = divmod(g, 3)
+            w_raw = w_raw_pool.tile([P, PACK, DIM], BF16)
+            w_raws[g] = w_raw
+            skip = 64 if w == 2 else 0
+            if skip:
+                nc.gpsimd.memset(w_raw[0:skip, :, :], 0.0)
+            first = HALF_K * h + WINDOWS[w] + PACK * skip
+            last = HALF_K * h + WINDOWS[w] + PASS_K
+            nc.sync.dma_start(out=w_raw[skip:P, :, :], in_=w2[first:last, :].rearrange("(p t) n -> p t n", t=PACK))
+
+        gain_rows = keep.tile([P, PASS_K], BF16)
+        bias_row = keep.tile([P, DIM], BF16)
+        ones = keep.tile([P, P], BF16)
+        one = keep.tile([P, 1], F32)
+        one_root = keep.tile([P, 1], F32)
+        zero_rows = keep.tile([BATCH, BAND_LEN], F32, tag="normed")
+        nc.vector.memset(gain_rows[:], 0.0)
+        nc.vector.memset(zero_rows[:], 0.0)
+        nc.vector.memset(bias_row[:], 0.0)
+        nc.vector.memset(ones[:], 1.0)
+        nc.vector.memset(one[:], 1.0)
+        for row, vec in ((0, ln2_g), (32, ln2_b)):
+            for h in range(2):
+                both = vec[HALF_K * h : HALF_K * h + 2 * PASS_K].rearrange("(s p) -> s p", p=PASS_K)
+                nc.scalar.dma_start(out=gain_rows[row + 3 * h : row + 3 * h + 2, :], in_=both)
+                third = vec[HALF_K * h + WINDOWS[2] : HALF_K * (h + 1)].unsqueeze(0)
+                nc.scalar.dma_start(out=gain_rows[row + 3 * h + 2 : row + 3 * h + 3, :], in_=third)
+        nc.scalar.dma_start(out=bias_row[0:1, :], in_=b2.unsqueeze(0))
+        nc.scalar.dma_start(out=scratch[0:BATCH, :], in_=zero_rows[:])
+        nc.scalar.dma_start(out=scratch[P + BATCH : P + 2 * BATCH, :], in_=zero_rows[:])
+        for c in range(4):
+            load_image(c)
+        load_w(PASS_ORDER[0])
+        for c in range(4, CH):
+            load_image(c)
+        for m in range(4):
+            nc.sync.dma_start(out=tok_in[:, m, :], in_=token_rows(tok, m))
+        for g in PASS_ORDER[1:EARLY_W]:
+            load_w(g)
+
+        nc.scalar.activation(out=one_root[:], in_=one[:], func=ACT.Sqrt)
+
+        ident = keep.tile([P, P], F32)
+        make_identity(nc, ident[:])
+        nc.gpsimd.memset(detail[:, :, 0:PAD, :], 0.0)
+        nc.gpsimd.memset(detail[:, :, PAD + DETAIL_W : PADDED_W, :], 0.0)
+
+        ident_ihb = ident[:].rearrange("p (i h b) -> p i h b", i=GRID, h=2)
+        turn_order = keep.tile([P, P], F32)
+        nc.vector.tensor_copy(
+            out=turn_order[:].rearrange("p (h b i) -> p h b i", h=2, b=BATCH),
+            in_=ident[:].rearrange("p (i h b) -> p h b i", i=GRID, h=2),
+        )
+        own_bands = keep.tile([P, GRID, BATCH], F32)
+        near_bands = keep.tile([P, GRID, BATCH], F32)
+        nc.vector.tensor_tensor(out=own_bands[:], in0=ident_ihb[:, :, 0, :], in1=ident_ihb[:, :, 1, :], op=ALU.add)
+        nc.vector.tensor_copy(out=near_bands[:, 0:1, :], in_=own_bands[:, 0:1, :])
+        nc.vector.tensor_tensor(
+            out=near_bands[:, 1:GRID, :], in0=own_bands[:, 1:GRID, :], in1=ident_ihb[:, 0 : GRID - 1, 1, :], op=ALU.add
+        )
+        nc.vector.tensor_tensor(
+            out=near_bands[:, 0 : GRID - 1, :], in0=near_bands[:, 0 : GRID - 1, :], in1=ident_ihb[:, 1:GRID, 0, :], op=ALU.add
+        )
+        sum_own = keep.tile([P, P], F32)
+        sum_near = keep.tile([P, P], F32)
+        nc.vector.tensor_copy(
+            out=sum_own[:].rearrange("p (i h b) -> p i h b", i=GRID, h=2),
+            in_=own_bands[:].unsqueeze(2).to_broadcast([P, GRID, 2, BATCH]),
+        )
+        nc.vector.tensor_copy(
+            out=sum_near[:].rearrange("p (i h b) -> p i h b", i=GRID, h=2),
+            in_=near_bands[:].unsqueeze(2).to_broadcast([P, GRID, 2, BATCH]),
+        )
+        strip_sums = keep.tile([P, 2, 18], F32)
+        nc.vector.memset(strip_sums[:], 0.0)
+
+        gain_f32 = keep.tile([P, PASS_K], F32)
+        nc.vector.tensor_copy(out=gain_f32[:], in_=gain_rows[:])
+        gain_ps = turn_psum.tile([P, PACK, P], F32, tag="turned")
+        for t in range(PACK):
+            nc.tensor.transpose(out=gain_ps[:, t, :], in_=gain_f32[:, t : t + PASS_K - PACK + 1 : PACK], identity=ident[:])
+        gain_t = keep.tile([P, PACK, P], F32)
+        nc.vector.tensor_copy(out=gain_t[:], in_=gain_ps[:])
+
+        bias_wide = acc_psum.tile([P, N_WIDE], F32, tag="wide0")
+        bias_rest = acc_psum.tile([P, DIM - N_WIDE], F32, tag="rest0")
+        nc.tensor.matmul(out=bias_wide[:], lhsT=ones[:], rhs=bias_row[:, 0:N_WIDE], start=True, stop=True)
+        nc.tensor.matmul(out=bias_rest[:], lhsT=ones[:], rhs=bias_row[:, N_WIDE:DIM], start=True, stop=True)
+
+        def add_bias(m):
+            nc.vector.tensor_tensor(out=tok_bias[:, m, 0:N_WIDE], in0=bias_wide[:], in1=tok_in[:, m, 0:N_WIDE], op=ALU.add)
+            nc.vector.tensor_tensor(out=tok_bias[:, m, N_WIDE:DIM], in0=bias_rest[:], in1=tok_in[:, m, N_WIDE:DIM], op=ALU.add)
+
+        w_grps = {}
+
+        def regroup_w(g, cols):
+            if g not in w_grps:
+                w_grp = w_grp_pool.tile([P, DIM, PACK], BF16, align_bytes=64)
+                w_grps[g] = w_grp
+            grouped = w_grps[g][:, cols, :].rearrange("p (n i) t -> p n t i", i=4)
+            rows = w_raws[g][:, :, cols].rearrange("p t (n i) -> p n t i", i=4)
+            if g == PASS_ORDER[-1]:
+                nc.vector.tensor_copy(out=grouped, in_=rows)
+            else:
+                nc.scalar.copy(out=grouped, in_=rows)
+
+        def quantise_w(g):
+            for cols in (WIDE, REST):
+                nc.vector.quantize_mx(
+                    out=w_codes[:, g, cols].bitcast(FP8X4),
+                    scales=w_scales[:, g, cols],
+                    in_=w_grps[g][:, cols, :].rearrange("p n t -> p (n t)"),
+                )
+
+        pixels = image[:].rearrange("p c (r u j v) -> p c r u j v", r=BAND_ROWS, u=2, j=DETAIL_W, v=2)
+        by_channel = keep.tile([P, CH, BAND_ROWS, DETAIL_W], F32)
+        bottom = keep.tile([P, CH, BAND_ROWS, DETAIL_W], F32)
+        squares = keep.tile([P, CH, BAND_ROWS, DETAIL_W], F32)
+        def rows_of_blocks(c):
+            pair = slice(c, c + 2)
+            nc.vector.scalar_tensor_tensor(
+                out=by_channel[:, pair, :, :],
+                in0=pixels[:, pair, :, 0, :, 0],
+                scalar=3.0,
+                in1=pixels[:, pair, :, 0, :, 1],
+                op0=ALU.mult,
+                op1=ALU.subtract,
+            )
+            nc.vector.tensor_tensor(
+                out=bottom[:, pair, :, :], in0=pixels[:, pair, :, 1, :, 0], in1=pixels[:, pair, :, 1, :, 1], op=ALU.add
+            )
+
+        def join_rows(c):
+            pair = slice(c, c + 2)
+            nc.vector.tensor_tensor(
+                out=by_channel[:, pair, :, :], in0=by_channel[:, pair, :, :], in1=bottom[:, pair, :, :], op=ALU.subtract
+            )
+            nc.scalar.activation(out=squares[:, pair, :, :], in_=by_channel[:, pair, :, :], func=ACT.Square)
+
+        for c in range(0, CH, 2):
+            rows_of_blocks(c)
+            if c > 0:
+                join_rows(c - 2)
+            if c == 4:
+                regroup_w(PASS_ORDER[0], WIDE)
+                regroup_w(PASS_ORDER[0], REST)
+        join_rows(CH - 2)
+        for r in range(BAND_ROWS):
+            sorted_row = detail[:, r, PAD : PAD + DETAIL_W, :].rearrange("p j (h c) -> p h j c", h=2)
+            row_by_channel = by_channel[:, :, r, :].rearrange("p (h c) j -> p h j c", h=2)
+            cols = slice(r * ROW_LEN, (r + 1) * ROW_LEN)
+            if r % 2 == 0:
+                nc.scalar.copy(out=sorted_row, in_=row_by_channel)
+                nc.scalar.dma_start(out=scratch[BATCH : BATCH + P, cols], in_=detail[:, r, :, :].rearrange("p j c -> p (j c)"))
+            else:
+                nc.vector.tensor_copy(out=sorted_row, in_=row_by_channel)
+                nc.sync.dma_start(out=scratch[BATCH : BATCH + P, cols], in_=detail[:, r, :, :].rearrange("p j c -> p (j c)"))
+        for r in range(BAND_ROWS):
+            cols = slice(r * ROW_LEN, (r + 1) * ROW_LEN)
+            nc.sync.dma_start(out=detail_up[:, r, :, :].rearrange("p j c -> p (j c)"), in_=scratch[0:P, cols])
+            nc.sync.dma_start(out=detail_dn[:, r, :, :].rearrange("p j c -> p (j c)"), in_=scratch[2 * BATCH : 2 * BATCH + P, cols])
+
+        nc.vector.tensor_reduce(
+            out=strip_sums[:, 0, 1:17], in_=by_channel[:].rearrange("p c r (e l) -> p e (c r) l", l=PAD), axis=AX.XY, op=ALU.add
+        )
+        nc.vector.tensor_reduce(
+            out=strip_sums[:, 1, 1:17], in_=squares[:].rearrange("p c r (e l) -> p e (c r) l", l=PAD), axis=AX.XY, op=ALU.add
+        )
+        window_sums = keep.tile([P, 2, 2, GRID], F32)
+        inner = strip_sums[:, :, 1:17].rearrange("p q (j v) -> p q j v", v=2)
+        left = strip_sums[:, :, 0:16].rearrange("p q (j v) -> p q j v", v=2)
+        right = strip_sums[:, :, 2:18].rearrange("p q (j v) -> p q j v", v=2)
+        nc.vector.tensor_tensor(out=window_sums[:, 0, :, :], in0=inner[:, :, :, 0], in1=inner[:, :, :, 1], op=ALU.add)
+        nc.vector.tensor_tensor(out=window_sums[:, 1, :, :], in0=left[:, :, :, 0], in1=right[:, :, :, 1], op=ALU.add)
+        nc.vector.tensor_tensor(out=window_sums[:, 1, :, :], in0=window_sums[:, 1, :, :], in1=window_sums[:, 0, :, :], op=ALU.add)
+        token_sums = turn_psum.tile([P, 2 * GRID], F32, tag="turned")
+        nc.tensor.matmul(
+            out=token_sums[:], lhsT=sum_own[:], rhs=window_sums[:, 0, :, :].rearrange("p q j -> p (q j)"), start=True, stop=False
+        )
+        nc.tensor.matmul(
+            out=token_sums[:], lhsT=sum_near[:], rhs=window_sums[:, 1, :, :].rearrange("p q j -> p (q j)"), start=False, stop=True
+        )
+        regroup_w(PASS_ORDER[1], WIDE)
+        add_bias(0)
+        mean = keep.tile([P, GRID], F32)
+        mean_sq = keep.tile([P, GRID], F32)
+        var = keep.tile([P, GRID], F32)
+        std = keep.tile([P, GRID], F32)
+        rstd0 = keep.tile([P, GRID], F32)
+        newton = keep.tile([P, GRID], F32)
+        rstd = keep.tile([P, GRID], F32)
+        shift = keep.tile([P, GRID], F32)
+        nc.vector.tensor_scalar(out=mean[:], in0=token_sums[:, 0:GRID], scalar1=1.0 / K, scalar2=None, op0=ALU.mult)
+        nc.vector.tensor_tensor(out=mean_sq[:], in0=mean[:], in1=mean[:], op=ALU.mult)
+        nc.vector.scalar_tensor_tensor(
+            out=var[:], in0=token_sums[:, GRID : 2 * GRID], scalar=1.0 / K, in1=mean_sq[:], op0=ALU.mult, op1=ALU.subtract
+        )
+        nc.vector.tensor_scalar(out=var[:], in0=var[:], scalar1=EPS, scalar2=None, op0=ALU.add)
+        nc.scalar.activation(out=std[:], in_=var[:], func=ACT.Sqrt)
+        add_bias(1)
+        nc.vector.reciprocal(out=rstd0[:], in_=std[:])
+        nc.vector.tensor_tensor(out=newton[:], in0=var[:], in1=rstd0[:], op=ALU.mult)
+        nc.vector.tensor_tensor(out=newton[:], in0=newton[:], in1=rstd0[:], op=ALU.mult)
+        nc.vector.tensor_scalar(out=newton[:], in0=newton[:], scalar1=-0.5, scalar2=1.5, op0=ALU.mult, op1=ALU.add)
+        nc.vector.tensor_tensor(out=rstd[:], in0=rstd0[:], in1=newton[:], op=ALU.mult)
+        nc.vector.scalar_tensor_tensor(out=shift[:], in0=mean[:], scalar=-1.0, in1=rstd[:], op0=ALU.mult, op1=ALU.mult)
+        regroup_w(PASS_ORDER[1], REST)
+        for g in PASS_ORDER[EARLY_W:]:
+            load_w(g)
+        regroup_w(PASS_ORDER[2], WIDE)
+        regroup_w(PASS_ORDER[2], REST)
+        quantise_w(PASS_ORDER[0])
+        add_bias(2)
+        add_bias(3)
+        quantise_w(PASS_ORDER[1])
+
+        normed = keep.tile([P, GRID, HALF_K], F32, tag="normed")
+        normed_v = normed[:].rearrange("p j (r q s c) -> p j r q s c", r=BAND_ROWS, q=PATCH, s=VIEWS, c=CH)
+        views = ((detail, 0), (detail_up, -PAD), (detail_up, PAD), (detail_dn, -PAD), (detail_dn, PAD))
+        planes = keep.tile([P, SLOTS, J_GROUPS, GROUP_TOKENS], BF16, tag="image")
+
+        def normalise(jq, s):
+            source, dx = views[s]
+            for j in range(jq * J_GROUP, (jq + 1) * J_GROUP):
+                first = PAD + PATCH * j + dx
+                if s == 0:
+                    nc.scalar.activation(
+                        out=normed_v[:, j, :, :, s, :],
+                        in_=source[:, :, first : first + PATCH, :],
+                        func=ACT.Identity,
+                        scale=rstd[:, j : j + 1],
+                        bias=shift[:, j : j + 1],
+                    )
+                else:
+                    nc.vector.tensor_scalar(
+                        out=normed_v[:, j, :, :, s, :],
+                        in0=source[:, :, first : first + PATCH, :],
+                        scalar1=rstd[:, j : j + 1],
+                        scalar2=shift[:, j : j + 1],
+                        op0=ALU.mult,
+                        op1=ALU.add,
+                    )
+
+        turned_tiles = {}
+
+        def turn(n):
+            jq, sg = divmod(n, HALF_SLOTS)
+            turned = turn_psum.tile([P, J_GROUP, P], F32)
+            turned_tiles[n] = turned
+            for j4 in range(J_GROUP):
+                w, t = divmod(sg, PACK)
+                first = WINDOWS[w] + t
+                nc.tensor.transpose(
+                    out=turned[:, j4, :],
+                    in_=normed[:, jq * J_GROUP + j4, first : first + PASS_K - PACK + 1 : PACK],
+                    identity=turn_order[:],
+                )
+
+        def empty(n):
+            jq, sg = divmod(n, HALF_SLOTS)
+            for h in range(2):
+                w, t = divmod(sg, PACK)
+                g = 3 * h + w
+                slot = PACK * g + t
+                nc.scalar.activation(
+                    out=planes[:, slot, jq, :].rearrange("p (g j) -> p g j", j=J_GROUP),
+                    in_=turned_tiles[n][:, :, 64 * h : 64 * h + 64].rearrange("p j g -> p g j"),
+                    func=ACT.Identity,
+                    scale=gain_t[:, t, g : g + 1],
+                    bias=gain_t[:, t, 32 + g : 33 + g],
+                )
+
+        z_grps = {}
+
+        def regroup_z(jq, g):
+            z_grp = z_grp_pool.tile([P, GROUP_TOKENS, PACK], BF16, align_bytes=64)
+            z_grps[(jq, g)] = z_grp
+            nc.vector.tensor_copy(
+                out=z_grp[:].rearrange("p (w i) t -> p w t i", i=4),
+                in_=planes[:, PACK * g : PACK * (g + 1), jq, :].rearrange("p t (w i) -> p w t i", i=4),
+            )
+
+        def quantise_z(jq, g):
+            toks = slice(jq * GROUP_TOKENS, (jq + 1) * GROUP_TOKENS)
+            nc.vector.quantize_mx(
+                out=z_codes[:, g, toks].bitcast(FP8X4),
+                scales=z_scales[:, g, toks],
+                in_=z_grps[(jq, g)][:].rearrange("p w t -> p (w t)"),
+            )
+
+        def passes_done_at(n):
+            jq, sg = divmod(n, HALF_SLOTS)
+            if not 0 <= n < STEPS or sg % PACK != PACK - 1:
+                return []
+            return [(jq, 3 * h + sg // PACK) for h in range(2)]
+
+        accs = {}
+
+        def multiply(jq, g):
+            for bh in range(2):
+                m = 2 * jq + bh
+                rows = slice(m * P, (m + 1) * P)
+                if g == PASS_ORDER[0]:
+                    acc_wide = acc_psum.tile([P, N_WIDE], F32, tag="wide%d" % bh)
+                    acc_rest = acc_psum.tile([P, DIM - N_WIDE], F32, tag="rest%d" % bh)
+                    accs[m] = ((acc_wide, WIDE), (acc_rest, REST))
+                for acc, cols in accs[m]:
+                    nc.tensor.matmul_mx(
+                        out=acc[:],
+                        lhsT=z_codes[:, g, rows].bitcast(FP8X4),
+                        lhsT_scale=z_scales[:, g, rows],
+                        rhs=w_codes[:, g, cols].bitcast(FP8X4),
+                        rhs_scale=w_scales[:, g, cols],
+                        start=(g == PASS_ORDER[0]),
+                        stop=(g == PASS_ORDER[-1]),
+                    )
+                if g == PASS_ORDER[-1]:
+                    for acc, cols in accs[m]:
+                        nc.vector.tensor_tensor(out=tok_bias[:, m, cols], in0=acc[:], in1=tok_bias[:, m, cols], op=ALU.add)
+                    nc.sync.dma_start(out=token_rows(out, m), in_=tok_bias[:, m, :])
+
+        normalise(0, 0)
+        normalise(1, 0)
+        regroup_w(PASS_ORDER[3], WIDE)
+        regroup_w(PASS_ORDER[3], REST)
+        quantise_w(PASS_ORDER[2])
+        for jq in range(J_GROUPS):
+            for s in range(1, VIEWS):
+                normalise(jq, s)
+        quantise_w(PASS_ORDER[3])
+        for n in range(AHEAD):
+            turn(n)
+        for n in range(STEPS + LAG):
+            if n + AHEAD < STEPS:
+                turn(n + AHEAD)
+            if n < STEPS:
+                empty(n)
+            for jq, g in passes_done_at(n):
+                regroup_z(jq, g)
+            for jq, g in passes_done_at(n - 1):
+                quantise_z(jq, g)
+            if n == LAST_W_STEP:
+                for g in PASS_ORDER[EARLY_W:]:
+                    regroup_w(g, WIDE)
+                    regroup_w(g, REST)
+                    quantise_w(g)
+            for jq, g in passes_done_at(n - LAG):
+                multiply(jq, g)

@@ -14,184 +14,150 @@ AX = mybir.AxisListType
 
 P = 128
 BATCH = 8
-CH = 8
-BANDS = 16
-BAND_ROWS = 4
-DETAIL_W = 64
-PAD = 4
-PADDED_W = DETAIL_W + 2 * PAD
-ROW_LEN = PADDED_W * CH
-BAND_LEN = BAND_ROWS * ROW_LEN
+CH_HALVES = 2
+CH = 4
+GROUPS = BATCH * CH_HALVES
 GRID = 8
 PATCH = 8
 VIEWS = 5
-HALF_K = BAND_ROWS * PATCH * VIEWS * CH
-K = 2 * HALF_K
+SHIFT = 4
+DETAIL_W = 64
+PADDED_W = DETAIL_W + 2 * SHIFT
+ROW_PIX = 128
+HALVES = 2
+HALF_ROWS = 4
+BANK_ROWS = 2
+K = PATCH * PATCH * VIEWS * CH * CH_HALVES
 DIM = 768
-TOKENS = BATCH * GRID * GRID
 PACK = 4
 PASS_K = P * PACK
-WINDOWS = (0, 512, 768)
-PASSES = 2 * len(WINDOWS)
-SLOTS = PASSES * PACK
-HALF_SLOTS = SLOTS // 2
+PASSES = K // PASS_K
+PLANE_LEN = PASSES * P
+PLANE_PITCH = 704
+UNIT = 4
+PAIR = VIEWS * UNIT
 J_GROUP = 4
 J_GROUPS = GRID // J_GROUP
-GROUP_TOKENS = TOKENS // J_GROUPS
+J_TILE = 2
+TILES = J_GROUP // J_TILE
+GROUP_TOKENS = BATCH * GRID * J_GROUP
 N_WIDE = 512
 WIDE = slice(0, N_WIDE)
 REST = slice(N_WIDE, DIM)
-PASS_ORDER = [3 * h + w for w in range(3) for h in range(2)]
-STEPS = J_GROUPS * HALF_SLOTS
 TURN_BANKS = 4
-AHEAD = TURN_BANKS - 1
-LAG = 6
-LAST_W_STEP = 6
-EARLY_W = 4
 HAAR_SCALE = 6.0
 EPS = 1e-5 * HAAR_SCALE * HAAR_SCALE
+STRIPS = DETAIL_W // SHIFT
+STRIP_HALF = HALF_ROWS * SHIFT * CH // 2
 
-FLOPS = 2 * TOKENS * K * DIM
+FLOPS = 2 * BATCH * GRID * GRID * K * DIM
 
 
 def tile_shiftedpatchtokenization_pb_kernel(tc, x, ln2_g, ln2_b, w2, b2, tok, out):
     nc = tc.nc
     with ExitStack() as ctx:
         keep = ctx.enter_context(tc.tile_pool(name="keep", bufs=1))
-        w_raw_pool = ctx.enter_context(tc.tile_pool(name="w_raw", bufs=EARLY_W))
+        w_raw_pool = ctx.enter_context(tc.tile_pool(name="w_raw", bufs=PASSES))
         w_grp_pool = ctx.enter_context(tc.tile_pool(name="w_grp", bufs=3))
         z_grp_pool = ctx.enter_context(tc.tile_pool(name="z_grp", bufs=3))
         turn_psum = ctx.enter_context(tc.psum_pool(name="turn_psum", bufs=TURN_BANKS))
         acc_psum = ctx.enter_context(tc.psum_pool(name="acc_psum", bufs=1))
         ctx.enter_context(tc.manual_schedule())
 
-        image = keep.tile([P, CH, 8 * 128], BF16, tag="image")
-        w_raws = {}
+        images = [keep.tile([P, CH, HALF_ROWS * 2 * ROW_PIX], BF16, name="image%d" % hr) for hr in range(HALVES)]
+        detail = keep.tile([P, PATCH, PADDED_W, CH], F32)
+        above = keep.tile([P, HALF_ROWS, PADDED_W, CH], F32)
+        below = keep.tile([P, HALF_ROWS, PADDED_W, CH], F32)
         w_codes = keep.tile([P, PASSES, DIM], U32, align_bytes=64)
         w_scales = keep.tile([P, PASSES, DIM], U8, align_bytes=64)
-        z_codes = keep.tile([P, PASSES, TOKENS], U32, align_bytes=64)
-        z_scales = keep.tile([P, PASSES, TOKENS], U8, align_bytes=64)
+        z_codes = keep.tile([P, PASSES, J_GROUPS * GROUP_TOKENS], U32, align_bytes=64)
+        z_scales = keep.tile([P, PASSES, J_GROUPS * GROUP_TOKENS], U8, align_bytes=64)
         tok_in = keep.tile([P, 4, DIM], BF16)
         tok_bias = keep.tile([P, 4, DIM], F32)
-        detail = keep.tile([P, BAND_ROWS, PADDED_W, CH], F32)
-        detail_up = keep.tile([P, BAND_ROWS, PADDED_W, CH], F32)
-        detail_dn = keep.tile([P, BAND_ROWS, PADDED_W, CH], F32)
-        scratch = out.rearrange("b n d -> (b n d)")[0 : (P + 2 * BATCH) * BAND_LEN].rearrange("(q f) -> q f", f=BAND_LEN)
+        normed = keep.tile([P, GRID * 2 * PLANE_PITCH + 2 * PAIR], F32, align_bytes=64)
+        planes = keep.tile([P, PASSES, PACK, J_GROUPS, GROUP_TOKENS], BF16)
 
         def token_rows(dram, m):
-            jq, bh = divmod(m, 2)
-            rows = dram[4 * bh : 4 * bh + 4, :, :]
-            return rows.rearrange("b (i q j) d -> q (b i) j d", q=J_GROUPS, j=J_GROUP)[jq]
+            return dram.rearrange("b (i q j) d -> q (b i) j d", q=4, j=J_TILE)[m]
 
-        def load_image(c):
-            nc.sync.dma_start(out=image[:, c, :], in_=x[:, c, :, :].rearrange("b (a r) w -> a b (r w)", a=BANDS))
+        x_parts = x.rearrange("b (h c) (i r) w -> c (b h) i (r w)", h=CH_HALVES, i=GRID)
+        w_parts = w2.rearrange("(g a t e) n -> g t a e n", g=PASSES, t=PACK, e=4)
+        half_pix = HALF_ROWS * 2 * ROW_PIX
+        w_raws = {}
+
+        def load_image(hr, c):
+            pix = slice(hr * half_pix, (hr + 1) * half_pix)
+            nc.sync.dma_start(out=images[hr][:, c, :], in_=x_parts[c][:, :, pix])
 
         def load_w(g):
-            h, w = divmod(g, 3)
             w_raw = w_raw_pool.tile([P, PACK, DIM], BF16)
             w_raws[g] = w_raw
-            skip = 64 if w == 2 else 0
-            if skip:
-                nc.gpsimd.memset(w_raw[0:skip, :, :], 0.0)
-            first = HALF_K * h + WINDOWS[w] + PACK * skip
-            last = HALF_K * h + WINDOWS[w] + PASS_K
-            nc.sync.dma_start(out=w_raw[skip:P, :, :], in_=w2[first:last, :].rearrange("(p t) n -> p t n", t=PACK))
+            for t in range(PACK):
+                nc.sync.dma_start(out=w_raw[:, t, :], in_=w_parts[g][t])
 
-        gain_rows = keep.tile([P, PASS_K], BF16)
-        bias_row = keep.tile([P, DIM], BF16)
-        ones = keep.tile([P, P], BF16)
-        one = keep.tile([P, 1], F32)
-        one_root = keep.tile([P, 1], F32)
-        zero_rows = keep.tile([BATCH, BAND_LEN], F32, tag="normed")
-        nc.vector.memset(gain_rows[:], 0.0)
-        nc.vector.memset(zero_rows[:], 0.0)
-        nc.vector.memset(bias_row[:], 0.0)
-        nc.vector.memset(ones[:], 1.0)
-        nc.vector.memset(one[:], 1.0)
-        for row, vec in ((0, ln2_g), (32, ln2_b)):
-            for h in range(2):
-                both = vec[HALF_K * h : HALF_K * h + 2 * PASS_K].rearrange("(s p) -> s p", p=PASS_K)
-                nc.scalar.dma_start(out=gain_rows[row + 3 * h : row + 3 * h + 2, :], in_=both)
-                third = vec[HALF_K * h + WINDOWS[2] : HALF_K * (h + 1)].unsqueeze(0)
-                nc.scalar.dma_start(out=gain_rows[row + 3 * h + 2 : row + 3 * h + 3, :], in_=third)
-        nc.scalar.dma_start(out=bias_row[0:1, :], in_=b2.unsqueeze(0))
-        nc.scalar.dma_start(out=scratch[0:BATCH, :], in_=zero_rows[:])
-        nc.scalar.dma_start(out=scratch[P + BATCH : P + 2 * BATCH, :], in_=zero_rows[:])
-        for c in range(4):
-            load_image(c)
-        load_w(PASS_ORDER[0])
-        for c in range(4, CH):
-            load_image(c)
-        for m in range(4):
+        def load_tok(m):
             nc.sync.dma_start(out=tok_in[:, m, :], in_=token_rows(tok, m))
-        for g in PASS_ORDER[1:EARLY_W]:
-            load_w(g)
 
-        nc.scalar.activation(out=one_root[:], in_=one[:], func=ACT.Sqrt)
+        rows_in = keep.tile([P, PASS_K + P], BF16)
+        nc.vector.memset(rows_in[:], 0.0)
+        for c in range(CH):
+            load_image(0, c)
+        for c in range(CH):
+            load_image(1, c)
+        load_w(0)
+        nc.scalar.dma_start(out=rows_in[0:PASSES, 0:PASS_K], in_=ln2_g.rearrange("(g k) -> g k", k=PASS_K))
+        nc.scalar.dma_start(out=rows_in[32 : 32 + PASSES, 0:PASS_K], in_=ln2_b.rearrange("(g k) -> g k", k=PASS_K))
+        nc.scalar.dma_start(out=rows_in[0 : DIM // P, PASS_K:], in_=b2.rearrange("(s p) -> s p", p=P))
 
         ident = keep.tile([P, P], F32)
         make_identity(nc, ident[:])
-        nc.gpsimd.memset(detail[:, :, 0:PAD, :], 0.0)
-        nc.gpsimd.memset(detail[:, :, PAD + DETAIL_W : PADDED_W, :], 0.0)
+        one = keep.tile([P, 1], F32)
+        one_root = keep.tile([P, 1], F32)
+        nc.gpsimd.memset(one[:], 1.0)
+        nc.scalar.activation(out=one_root[:], in_=one[:], func=ACT.Sqrt)
+        strips = keep.tile([P, HALVES, 2, 18], F32)
+        nc.gpsimd.memset(detail[:, :, 0:SHIFT, :], 0.0)
+        nc.gpsimd.memset(detail[:, :, SHIFT + DETAIL_W : PADDED_W, :], 0.0)
+        nc.gpsimd.memset(above[:], 0.0)
+        nc.gpsimd.memset(below[:], 0.0)
+        nc.gpsimd.memset(strips[:], 0.0)
 
-        ident_ihb = ident[:].rearrange("p (i h b) -> p i h b", i=GRID, h=2)
+        neg_ident = keep.tile([P, P], BF16)
+        nc.vector.tensor_scalar(out=neg_ident[:], in0=ident[:], scalar1=-1.0, scalar2=None, op0=ALU.mult)
         turn_order = keep.tile([P, P], F32)
+        ident_v = ident[:].rearrange("p (b h i) -> p b h i", h=CH_HALVES, i=GRID)
         nc.vector.tensor_copy(
-            out=turn_order[:].rearrange("p (h b i) -> p h b i", h=2, b=BATCH),
-            in_=ident[:].rearrange("p (i h b) -> p h b i", i=GRID, h=2),
+            out=turn_order[:].rearrange("p (h b i) -> p b h i", h=CH_HALVES, i=GRID),
+            in_=ident_v,
         )
-        own_bands = keep.tile([P, GRID, BATCH], F32)
-        near_bands = keep.tile([P, GRID, BATCH], F32)
-        nc.vector.tensor_tensor(out=own_bands[:], in0=ident_ihb[:, :, 0, :], in1=ident_ihb[:, :, 1, :], op=ALU.add)
-        nc.vector.tensor_copy(out=near_bands[:, 0:1, :], in_=own_bands[:, 0:1, :])
-        nc.vector.tensor_tensor(
-            out=near_bands[:, 1:GRID, :], in0=own_bands[:, 1:GRID, :], in1=ident_ihb[:, 0 : GRID - 1, 1, :], op=ALU.add
+        row_sum = keep.tile([P, BATCH, GRID + 2], F32)
+        nc.vector.memset(row_sum[:], 0.0)
+        nc.vector.tensor_tensor(out=row_sum[:, :, 1 : GRID + 1], in0=ident_v[:, :, 0, :], in1=ident_v[:, :, 1, :], op=ALU.add)
+        nc.vector.tensor_scalar(
+            out=row_sum[:, :, 1 : GRID + 1], in0=row_sum[:, :, 1 : GRID + 1], scalar1=1.0 / K, scalar2=None, op0=ALU.mult
         )
-        nc.vector.tensor_tensor(
-            out=near_bands[:, 0 : GRID - 1, :], in0=near_bands[:, 0 : GRID - 1, :], in1=ident_ihb[:, 1:GRID, 0, :], op=ALU.add
-        )
-        sum_own = keep.tile([P, P], F32)
-        sum_near = keep.tile([P, P], F32)
-        nc.vector.tensor_copy(
-            out=sum_own[:].rearrange("p (i h b) -> p i h b", i=GRID, h=2),
-            in_=own_bands[:].unsqueeze(2).to_broadcast([P, GRID, 2, BATCH]),
-        )
-        nc.vector.tensor_copy(
-            out=sum_near[:].rearrange("p (i h b) -> p i h b", i=GRID, h=2),
-            in_=near_bands[:].unsqueeze(2).to_broadcast([P, GRID, 2, BATCH]),
-        )
-        strip_sums = keep.tile([P, 2, 18], F32)
-        nc.vector.memset(strip_sums[:], 0.0)
-
-        gain_f32 = keep.tile([P, PASS_K], F32)
-        nc.vector.tensor_copy(out=gain_f32[:], in_=gain_rows[:])
-        gain_ps = turn_psum.tile([P, PACK, P], F32, tag="turned")
-        for t in range(PACK):
-            nc.tensor.transpose(out=gain_ps[:, t, :], in_=gain_f32[:, t : t + PASS_K - PACK + 1 : PACK], identity=ident[:])
-        gain_t = keep.tile([P, PACK, P], F32)
-        nc.vector.tensor_copy(out=gain_t[:], in_=gain_ps[:])
-
-        bias_wide = acc_psum.tile([P, N_WIDE], F32, tag="wide0")
-        bias_rest = acc_psum.tile([P, DIM - N_WIDE], F32, tag="rest0")
-        nc.tensor.matmul(out=bias_wide[:], lhsT=ones[:], rhs=bias_row[:, 0:N_WIDE], start=True, stop=True)
-        nc.tensor.matmul(out=bias_rest[:], lhsT=ones[:], rhs=bias_row[:, N_WIDE:DIM], start=True, stop=True)
-
-        def add_bias(m):
-            nc.vector.tensor_tensor(out=tok_bias[:, m, 0:N_WIDE], in0=bias_wide[:], in1=tok_in[:, m, 0:N_WIDE], op=ALU.add)
-            nc.vector.tensor_tensor(out=tok_bias[:, m, N_WIDE:DIM], in0=bias_rest[:], in1=tok_in[:, m, N_WIDE:DIM], op=ALU.add)
+        sum_mats = []
+        for name, first in (("own", 1), ("above", 0), ("below", 2)):
+            mat = keep.tile([P, P], F32, name="sum_%s" % name)
+            nc.vector.tensor_copy(
+                out=mat[:].rearrange("p (b h i) -> p b h i", h=CH_HALVES, i=GRID),
+                in_=row_sum[:, :, first : first + GRID].unsqueeze(2).to_broadcast([P, BATCH, CH_HALVES, GRID]),
+            )
+            sum_mats.append(mat)
+        sum_own, sum_above, sum_below = sum_mats
 
         w_grps = {}
 
-        def regroup_w(g, cols):
+        def regroup_w(engine, g, cols):
             if g not in w_grps:
                 w_grp = w_grp_pool.tile([P, DIM, PACK], BF16, align_bytes=64)
                 w_grps[g] = w_grp
             grouped = w_grps[g][:, cols, :].rearrange("p (n i) t -> p n t i", i=4)
             rows = w_raws[g][:, :, cols].rearrange("p t (n i) -> p n t i", i=4)
-            if g == PASS_ORDER[-1]:
-                nc.vector.tensor_copy(out=grouped, in_=rows)
-            else:
+            if engine == "scalar":
                 nc.scalar.copy(out=grouped, in_=rows)
+            else:
+                nc.vector.tensor_copy(out=grouped, in_=rows)
 
         def quantise_w(g):
             for cols in (WIDE, REST):
@@ -201,159 +167,227 @@ def tile_shiftedpatchtokenization_pb_kernel(tc, x, ln2_g, ln2_b, w2, b2, tok, ou
                     in_=w_grps[g][:, cols, :].rearrange("p n t -> p (n t)"),
                 )
 
-        pixels = image[:].rearrange("p c (r u j v) -> p c r u j v", r=BAND_ROWS, u=2, j=DETAIL_W, v=2)
-        by_channel = keep.tile([P, CH, BAND_ROWS, DETAIL_W], F32)
-        bottom = keep.tile([P, CH, BAND_ROWS, DETAIL_W], F32)
-        squares = keep.tile([P, CH, BAND_ROWS, DETAIL_W], F32)
-        def rows_of_blocks(c):
-            pair = slice(c, c + 2)
+        pixels = [t[:].rearrange("p c (r u j v) -> p c r u j v", r=HALF_ROWS, u=2, j=DETAIL_W, v=2) for t in images]
+        banks = {}
+
+        def haar_taps(bank, c):
+            if bank not in banks:
+                lower = turn_psum.tile([P, CH, BANK_ROWS, DETAIL_W], F32, tag="turned")
+                banks[bank] = lower
+            hr, first = divmod(bank * BANK_ROWS, HALF_ROWS)
+            taps = ((1, 0), (1, 1)) if bank == 0 else ((0, 1), (1, 0), (1, 1))
+            for n, (u, v) in enumerate(taps):
+                nc.tensor.matmul(
+                    out=banks[bank][:, c, :, :],
+                    lhsT=neg_ident[:],
+                    rhs=pixels[hr][:, c, first : first + BANK_ROWS, u, :, v],
+                    start=(n == 0),
+                    stop=(n == len(taps) - 1),
+                )
+
+        def haar_row(row, in1, op1):
             nc.vector.scalar_tensor_tensor(
-                out=by_channel[:, pair, :, :],
-                in0=pixels[:, pair, :, 0, :, 0],
+                out=detail[:, row, SHIFT : SHIFT + DETAIL_W, :],
+                in0=pixels[row // HALF_ROWS][:, :, row % HALF_ROWS, 0, :, 0].rearrange("p c j -> p j c"),
                 scalar=3.0,
-                in1=pixels[:, pair, :, 0, :, 1],
+                in1=in1.rearrange("p c j -> p j c"),
                 op0=ALU.mult,
-                op1=ALU.subtract,
-            )
-            nc.vector.tensor_tensor(
-                out=bottom[:, pair, :, :], in0=pixels[:, pair, :, 1, :, 0], in1=pixels[:, pair, :, 1, :, 1], op=ALU.add
+                op1=op1,
             )
 
-        def join_rows(c):
-            pair = slice(c, c + 2)
-            nc.vector.tensor_tensor(
-                out=by_channel[:, pair, :, :], in0=by_channel[:, pair, :, :], in1=bottom[:, pair, :, :], op=ALU.subtract
+        def haar_join(bank):
+            for r in range(BANK_ROWS):
+                haar_row(bank * BANK_ROWS + r, banks[bank][:, :, r, :], ALU.add)
+
+        def haar_first_bank():
+            for row in range(BANK_ROWS):
+                haar_row(row, pixels[0][:, :, row, 0, :, 1], ALU.subtract)
+            for row in range(BANK_ROWS):
+                inside = detail[:, row, SHIFT : SHIFT + DETAIL_W, :]
+                nc.vector.tensor_tensor(
+                    out=inside, in0=inside, in1=banks[0][:, :, row, :].rearrange("p c j -> p j c"), op=ALU.add
+                )
+
+        strip_stats = keep.tile([P, HALVES, STRIPS, 6], F32)
+
+        def strip_moments(hr):
+            for e in range(STRIPS):
+                cols = slice(SHIFT + e * SHIFT, SHIFT + (e + 1) * SHIFT)
+                nc.vector.bn_stats(
+                    out=strip_stats[:, hr, e, :],
+                    in_=detail[:, hr * HALF_ROWS : (hr + 1) * HALF_ROWS, cols, :].rearrange("p r l c -> p r (l c)"),
+                )
+
+        def send_below():
+            for i in range(GRID - 1):
+                nc.sync.dma_start(out=below[i:P:GRID, :, :, :], in_=detail[i + 1 : P : GRID, 0:HALF_ROWS, :, :])
+
+        def send_above():
+            for i in range(GRID - 1):
+                nc.sync.dma_start(out=above[i + 1 : P : GRID, :, :, :], in_=detail[i:P:GRID, HALF_ROWS:PATCH, :, :])
+
+        rows_f32 = keep.tile([P, PACK + 1, P], F32)
+        nc.vector.tensor_copy(
+            out=rows_f32[:, 0:PACK, :].rearrange("p t (a e) -> p a t e", e=4),
+            in_=rows_in[:, 0:PASS_K].rearrange("p (a t e) -> p a t e", t=PACK, e=4),
+        )
+        nc.vector.tensor_copy(out=rows_f32[:, PACK, :], in_=rows_in[:, PASS_K:])
+
+        for bank in (0, 1):
+            for c in range(CH):
+                haar_taps(bank, c)
+        haar_first_bank()
+        haar_join(1)
+        send_below()
+        load_w(1)
+        for bank in (2, 3):
+            for c in range(CH):
+                haar_taps(bank, c)
+        gain_ps = acc_psum.tile([P, PACK, P], F32, tag="wide0")
+        b2_ps = acc_psum.tile([P, P], F32, tag="rest0")
+        for t in range(PACK):
+            nc.tensor.transpose(out=gain_ps[:, t, :], in_=rows_f32[:, t, :], identity=ident[:])
+        nc.tensor.transpose(out=b2_ps[:], in_=rows_f32[:, PACK, :], identity=ident[:])
+        gain_t = keep.tile([P, PACK, P], F32)
+        b2_t = keep.tile([P, DIM // P], F32)
+        nc.scalar.copy(out=b2_t[:], in_=b2_ps[:, 0 : DIM // P])
+        nc.scalar.copy(out=gain_t[:], in_=gain_ps[:])
+        strip_moments(0)
+        haar_join(2)
+        haar_join(3)
+        send_above()
+        load_w(2)
+        for g in (3, 4):
+            load_w(g)
+        for m in range(4):
+            load_tok(m)
+        strip_moments(1)
+        b2_wide = acc_psum.tile([P, N_WIDE], F32, tag="wide1")
+        b2_rest = acc_psum.tile([P, DIM - N_WIDE], F32, tag="rest1")
+        for s in range(DIM // P):
+            bank, first = (b2_wide, 0) if s < N_WIDE // P else (b2_rest, N_WIDE // P)
+            nc.tensor.transpose(
+                out=bank[:, (s - first) * P : (s - first + 1) * P],
+                in_=b2_t[:, s : s + 1].to_broadcast([P, P]),
+                identity=ident[:],
             )
-            nc.scalar.activation(out=squares[:, pair, :, :], in_=by_channel[:, pair, :, :], func=ACT.Square)
+        b2_all = keep.tile([P, DIM], BF16)
 
-        for c in range(0, CH, 2):
-            rows_of_blocks(c)
-            if c > 0:
-                join_rows(c - 2)
-            if c == 4:
-                regroup_w(PASS_ORDER[0], WIDE)
-                regroup_w(PASS_ORDER[0], REST)
-        join_rows(CH - 2)
-        for r in range(BAND_ROWS):
-            sorted_row = detail[:, r, PAD : PAD + DETAIL_W, :].rearrange("p j (h c) -> p h j c", h=2)
-            row_by_channel = by_channel[:, :, r, :].rearrange("p (h c) j -> p h j c", h=2)
-            cols = slice(r * ROW_LEN, (r + 1) * ROW_LEN)
-            if r % 2 == 0:
-                nc.scalar.copy(out=sorted_row, in_=row_by_channel)
-                nc.scalar.dma_start(out=scratch[BATCH : BATCH + P, cols], in_=detail[:, r, :, :].rearrange("p j c -> p (j c)"))
-            else:
-                nc.vector.tensor_copy(out=sorted_row, in_=row_by_channel)
-                nc.sync.dma_start(out=scratch[BATCH : BATCH + P, cols], in_=detail[:, r, :, :].rearrange("p j c -> p (j c)"))
-        for r in range(BAND_ROWS):
-            cols = slice(r * ROW_LEN, (r + 1) * ROW_LEN)
-            nc.sync.dma_start(out=detail_up[:, r, :, :].rearrange("p j c -> p (j c)"), in_=scratch[0:P, cols])
-            nc.sync.dma_start(out=detail_dn[:, r, :, :].rearrange("p j c -> p (j c)"), in_=scratch[2 * BATCH : 2 * BATCH + P, cols])
+        def add_bias(m):
+            nc.vector.tensor_tensor(out=tok_bias[:, m, :], in0=tok_in[:, m, :], in1=b2_all[:], op=ALU.add)
 
-        nc.vector.tensor_reduce(
-            out=strip_sums[:, 0, 1:17], in_=by_channel[:].rearrange("p c r (e l) -> p e (c r) l", l=PAD), axis=AX.XY, op=ALU.add
+        regroup_w("scalar", 0, REST)
+        regroup_w("scalar", 0, WIDE)
+        nc.scalar.copy(out=b2_all[:, WIDE], in_=b2_wide[:])
+        nc.scalar.copy(out=b2_all[:, REST], in_=b2_rest[:])
+        regroup_w("scalar", 1, REST)
+        regroup_w("scalar", 1, slice(0, N_WIDE // 2))
+
+        stats = strip_stats[:].rearrange("p h e (o f) -> p (h e) o f", o=2)
+        mean_squares = keep.tile([P, HALVES * STRIPS, 2], F32)
+        square_sums = keep.tile([P, HALVES * STRIPS, 2], F32)
+        nc.vector.tensor_tensor(out=mean_squares[:], in0=stats[:, :, :, 1], in1=stats[:, :, :, 1], op=ALU.mult)
+        nc.vector.tensor_tensor(
+            out=strips[:, :, 0, 1 : 1 + STRIPS],
+            in0=strip_stats[:, :, :, 1],
+            in1=strip_stats[:, :, :, 4],
+            op=ALU.add,
         )
-        nc.vector.tensor_reduce(
-            out=strip_sums[:, 1, 1:17], in_=squares[:].rearrange("p c r (e l) -> p e (c r) l", l=PAD), axis=AX.XY, op=ALU.add
+        nc.vector.scalar_tensor_tensor(
+            out=square_sums[:], in0=mean_squares[:], scalar=float(STRIP_HALF), in1=stats[:, :, :, 2], op0=ALU.mult, op1=ALU.add
         )
-        window_sums = keep.tile([P, 2, 2, GRID], F32)
-        inner = strip_sums[:, :, 1:17].rearrange("p q (j v) -> p q j v", v=2)
-        left = strip_sums[:, :, 0:16].rearrange("p q (j v) -> p q j v", v=2)
-        right = strip_sums[:, :, 2:18].rearrange("p q (j v) -> p q j v", v=2)
-        nc.vector.tensor_tensor(out=window_sums[:, 0, :, :], in0=inner[:, :, :, 0], in1=inner[:, :, :, 1], op=ALU.add)
-        nc.vector.tensor_tensor(out=window_sums[:, 1, :, :], in0=left[:, :, :, 0], in1=right[:, :, :, 1], op=ALU.add)
-        nc.vector.tensor_tensor(out=window_sums[:, 1, :, :], in0=window_sums[:, 1, :, :], in1=window_sums[:, 0, :, :], op=ALU.add)
-        token_sums = turn_psum.tile([P, 2 * GRID], F32, tag="turned")
-        nc.tensor.matmul(
-            out=token_sums[:], lhsT=sum_own[:], rhs=window_sums[:, 0, :, :].rearrange("p q j -> p (q j)"), start=True, stop=False
-        )
-        nc.tensor.matmul(
-            out=token_sums[:], lhsT=sum_near[:], rhs=window_sums[:, 1, :, :].rearrange("p q j -> p (q j)"), start=False, stop=True
-        )
-        regroup_w(PASS_ORDER[1], WIDE)
-        add_bias(0)
+        pairs = square_sums[:].rearrange("p (h e) o -> p h e o", h=HALVES)
+        nc.vector.tensor_tensor(out=strips[:, :, 1, 1 : 1 + STRIPS], in0=pairs[:, :, :, 0], in1=pairs[:, :, :, 1], op=ALU.add)
+        inner = keep.tile([P, HALVES, 2, GRID], F32)
+        sides = keep.tile([P, HALVES, 2, GRID], F32)
+        mid = strips[:, :, :, 1:17].rearrange("p h q (j v) -> p h q j v", v=2)
+        left = strips[:, :, :, 0:16].rearrange("p h q (j v) -> p h q j v", v=2)
+        right = strips[:, :, :, 2:18].rearrange("p h q (j v) -> p h q j v", v=2)
+        nc.vector.tensor_tensor(out=inner[:], in0=mid[:, :, :, :, 0], in1=mid[:, :, :, :, 1], op=ALU.add)
+        nc.vector.tensor_tensor(out=sides[:], in0=left[:, :, :, :, 0], in1=right[:, :, :, :, 1], op=ALU.add)
+        outer = keep.tile([P, HALVES, 2, GRID], F32)
+        both = keep.tile([P, HALVES, 2, GRID], F32)
+        own = keep.tile([P, 2, GRID], F32)
+        nc.vector.tensor_tensor(out=outer[:], in0=sides[:], in1=inner[:], op=ALU.add)
+        nc.vector.tensor_tensor(out=both[:], in0=outer[:], in1=inner[:], op=ALU.add)
+        nc.vector.tensor_tensor(out=own[:], in0=both[:, 0, :, :], in1=both[:, 1, :, :], op=ALU.add)
+        moments = turn_psum.tile([P, 2, GRID], F32, tag="turned")
+        terms = ((sum_above, outer[:, 1, :, :]), (sum_below, outer[:, 0, :, :]), (sum_own, own[:]))
+        for n, (mat, sums) in enumerate(terms):
+            nc.tensor.matmul(
+                out=moments[:].rearrange("p q j -> p (q j)"),
+                lhsT=mat[:],
+                rhs=sums.rearrange("p q j -> p (q j)"),
+                start=(n == 0),
+                stop=(n == len(terms) - 1),
+            )
+        quantise_w(0)
         mean = keep.tile([P, GRID], F32)
         mean_sq = keep.tile([P, GRID], F32)
         var = keep.tile([P, GRID], F32)
         std = keep.tile([P, GRID], F32)
-        rstd0 = keep.tile([P, GRID], F32)
-        newton = keep.tile([P, GRID], F32)
         rstd = keep.tile([P, GRID], F32)
         shift = keep.tile([P, GRID], F32)
-        nc.vector.tensor_scalar(out=mean[:], in0=token_sums[:, 0:GRID], scalar1=1.0 / K, scalar2=None, op0=ALU.mult)
-        nc.vector.tensor_tensor(out=mean_sq[:], in0=mean[:], in1=mean[:], op=ALU.mult)
+        nc.scalar.activation(out=mean_sq[:], in_=moments[:, 0, :], func=ACT.Square, scale=float(STRIP_HALF))
+        nc.vector.tensor_scalar(out=mean[:], in0=moments[:, 0, :], scalar1=float(STRIP_HALF), scalar2=None, op0=ALU.mult)
         nc.vector.scalar_tensor_tensor(
-            out=var[:], in0=token_sums[:, GRID : 2 * GRID], scalar=1.0 / K, in1=mean_sq[:], op0=ALU.mult, op1=ALU.subtract
+            out=var[:], in0=moments[:, 1, :], scalar=EPS, in1=mean_sq[:], op0=ALU.add, op1=ALU.subtract
         )
-        nc.vector.tensor_scalar(out=var[:], in0=var[:], scalar1=EPS, scalar2=None, op0=ALU.add)
         nc.scalar.activation(out=std[:], in_=var[:], func=ACT.Sqrt)
-        add_bias(1)
-        nc.vector.reciprocal(out=rstd0[:], in_=std[:])
-        nc.vector.tensor_tensor(out=newton[:], in0=var[:], in1=rstd0[:], op=ALU.mult)
-        nc.vector.tensor_tensor(out=newton[:], in0=newton[:], in1=rstd0[:], op=ALU.mult)
-        nc.vector.tensor_scalar(out=newton[:], in0=newton[:], scalar1=-0.5, scalar2=1.5, op0=ALU.mult, op1=ALU.add)
-        nc.vector.tensor_tensor(out=rstd[:], in0=rstd0[:], in1=newton[:], op=ALU.mult)
+        nc.vector.reciprocal(out=rstd[:], in_=std[:])
         nc.vector.scalar_tensor_tensor(out=shift[:], in0=mean[:], scalar=-1.0, in1=rstd[:], op0=ALU.mult, op1=ALU.mult)
-        regroup_w(PASS_ORDER[1], REST)
-        for g in PASS_ORDER[EARLY_W:]:
-            load_w(g)
-        regroup_w(PASS_ORDER[2], WIDE)
-        regroup_w(PASS_ORDER[2], REST)
-        quantise_w(PASS_ORDER[0])
-        add_bias(2)
-        add_bias(3)
-        quantise_w(PASS_ORDER[1])
 
-        normed = keep.tile([P, GRID, HALF_K], F32, tag="normed")
-        normed_v = normed[:].rearrange("p j (r q s c) -> p j r q s c", r=BAND_ROWS, q=PATCH, s=VIEWS, c=CH)
-        views = ((detail, 0), (detail_up, -PAD), (detail_up, PAD), (detail_dn, -PAD), (detail_dn, PAD))
-        planes = keep.tile([P, SLOTS, J_GROUPS, GROUP_TOKENS], BF16, tag="image")
-
-        def normalise(jq, s):
-            source, dx = views[s]
-            for j in range(jq * J_GROUP, (jq + 1) * J_GROUP):
-                first = PAD + PATCH * j + dx
-                if s == 0:
+        def normalise(engine, j, s, parts=(0, 1)):
+            first = SHIFT + PATCH * j + (0, -SHIFT, SHIFT, -SHIFT, SHIFT)[s]
+            if s == 0:
+                pieces = ((detail, 0, 0, PATCH),)
+            elif s in (1, 2):
+                pieces = ((detail, 0, HALF_ROWS, HALF_ROWS), (above, 0, 0, HALF_ROWS))
+            else:
+                pieces = ((detail, HALF_ROWS, 0, HALF_ROWS), (below, 0, HALF_ROWS, HALF_ROWS))
+            base = 2 * PLANE_PITCH * j
+            if s % 2 == 0:
+                start, step = base + UNIT * (s // 2), PLANE_PITCH + 2 * UNIT
+            else:
+                start, step = base + UNIT * (s // 2 + 3), PLANE_PITCH - 3 * UNIT
+            target = normed[:, start : start + 2 * step].rearrange("p (l f) -> p l f", l=2)[:, :, 0:PLANE_LEN]
+            target = target.rearrange("p l (r h u) -> p r h l u", r=PATCH, u=PAIR)[:, :, :, :, 0:UNIT]
+            if s % 2 == 1:
+                target = target[:, :, :, ::-1, :]
+            for part in parts if s > 0 else (0,):
+                tile, row, to_row, count = pieces[part]
+                source = tile[:, row : row + count, first : first + PATCH, :].rearrange("p r (h l) c -> p r h l c", l=2)
+                goal = target[:, to_row : to_row + count, :, :, :]
+                if engine == "scalar":
                     nc.scalar.activation(
-                        out=normed_v[:, j, :, :, s, :],
-                        in_=source[:, :, first : first + PATCH, :],
-                        func=ACT.Identity,
-                        scale=rstd[:, j : j + 1],
-                        bias=shift[:, j : j + 1],
+                        out=goal, in_=source, func=ACT.Identity, scale=rstd[:, j : j + 1], bias=shift[:, j : j + 1]
                     )
                 else:
                     nc.vector.tensor_scalar(
-                        out=normed_v[:, j, :, :, s, :],
-                        in0=source[:, :, first : first + PATCH, :],
-                        scalar1=rstd[:, j : j + 1],
-                        scalar2=shift[:, j : j + 1],
-                        op0=ALU.mult,
-                        op1=ALU.add,
+                        out=goal,
+                        in0=source,
+                        scalar1=mean[:, j : j + 1],
+                        scalar2=rstd[:, j : j + 1],
+                        op0=ALU.subtract,
+                        op1=ALU.mult,
                     )
 
         turned_tiles = {}
 
-        def turn(n):
-            jq, sg = divmod(n, HALF_SLOTS)
+        def turn(jq, g, parity):
             turned = turn_psum.tile([P, J_GROUP, P], F32)
-            turned_tiles[n] = turned
+            turned_tiles[(jq, g, parity)] = turned
             for j4 in range(J_GROUP):
-                w, t = divmod(sg, PACK)
-                first = WINDOWS[w] + t
-                nc.tensor.transpose(
-                    out=turned[:, j4, :],
-                    in_=normed[:, jq * J_GROUP + j4, first : first + PASS_K - PACK + 1 : PACK],
-                    identity=turn_order[:],
-                )
+                first = PLANE_PITCH * (2 * (jq * J_GROUP + j4) + parity) + P * g
+                nc.tensor.transpose(out=turned[:, j4, :], in_=normed[:, first : first + P], identity=turn_order[:])
 
-        def empty(n):
-            jq, sg = divmod(n, HALF_SLOTS)
-            for h in range(2):
-                w, t = divmod(sg, PACK)
-                g = 3 * h + w
-                slot = PACK * g + t
+        def empty(jq, g, parity):
+            turned = turned_tiles[(jq, g, parity)][:].rearrange("p (m j) (h r) -> p h m r j", j=J_TILE, h=CH_HALVES)
+            for h in range(CH_HALVES):
+                t = 2 * parity + h
                 nc.scalar.activation(
-                    out=planes[:, slot, jq, :].rearrange("p (g j) -> p g j", j=J_GROUP),
-                    in_=turned_tiles[n][:, :, 64 * h : 64 * h + 64].rearrange("p j g -> p g j"),
+                    out=planes[:, g, t, jq, :].rearrange("p (m r j) -> p m r j", m=TILES, j=J_TILE),
+                    in_=turned[:, h, :, :, :],
                     func=ACT.Identity,
                     scale=gain_t[:, t, g : g + 1],
                     bias=gain_t[:, t, 32 + g : 33 + g],
@@ -366,7 +400,7 @@ def tile_shiftedpatchtokenization_pb_kernel(tc, x, ln2_g, ln2_b, w2, b2, tok, ou
             z_grps[(jq, g)] = z_grp
             nc.vector.tensor_copy(
                 out=z_grp[:].rearrange("p (w i) t -> p w t i", i=4),
-                in_=planes[:, PACK * g : PACK * (g + 1), jq, :].rearrange("p t (w i) -> p w t i", i=4),
+                in_=planes[:, g, :, jq, :].rearrange("p t (w i) -> p w t i", i=4),
             )
 
         def quantise_z(jq, g):
@@ -377,21 +411,15 @@ def tile_shiftedpatchtokenization_pb_kernel(tc, x, ln2_g, ln2_b, w2, b2, tok, ou
                 in_=z_grps[(jq, g)][:].rearrange("p w t -> p (w t)"),
             )
 
-        def passes_done_at(n):
-            jq, sg = divmod(n, HALF_SLOTS)
-            if not 0 <= n < STEPS or sg % PACK != PACK - 1:
-                return []
-            return [(jq, 3 * h + sg // PACK) for h in range(2)]
-
         accs = {}
 
         def multiply(jq, g):
-            for bh in range(2):
-                m = 2 * jq + bh
+            for tile in range(TILES):
+                m = TILES * jq + tile
                 rows = slice(m * P, (m + 1) * P)
-                if g == PASS_ORDER[0]:
-                    acc_wide = acc_psum.tile([P, N_WIDE], F32, tag="wide%d" % bh)
-                    acc_rest = acc_psum.tile([P, DIM - N_WIDE], F32, tag="rest%d" % bh)
+                if g == 0:
+                    acc_wide = acc_psum.tile([P, N_WIDE], F32, tag="wide%d" % tile)
+                    acc_rest = acc_psum.tile([P, DIM - N_WIDE], F32, tag="rest%d" % tile)
                     accs[m] = ((acc_wide, WIDE), (acc_rest, REST))
                 for acc, cols in accs[m]:
                     nc.tensor.matmul_mx(
@@ -400,38 +428,65 @@ def tile_shiftedpatchtokenization_pb_kernel(tc, x, ln2_g, ln2_b, w2, b2, tok, ou
                         lhsT_scale=z_scales[:, g, rows],
                         rhs=w_codes[:, g, cols].bitcast(FP8X4),
                         rhs_scale=w_scales[:, g, cols],
-                        start=(g == PASS_ORDER[0]),
-                        stop=(g == PASS_ORDER[-1]),
+                        start=(g == 0),
+                        stop=(g == PASSES - 1),
                     )
-                if g == PASS_ORDER[-1]:
-                    for acc, cols in accs[m]:
-                        nc.vector.tensor_tensor(out=tok_bias[:, m, cols], in0=acc[:], in1=tok_bias[:, m, cols], op=ALU.add)
-                    nc.sync.dma_start(out=token_rows(out, m), in_=tok_bias[:, m, :])
 
-        normalise(0, 0)
-        normalise(1, 0)
-        regroup_w(PASS_ORDER[3], WIDE)
-        regroup_w(PASS_ORDER[3], REST)
-        quantise_w(PASS_ORDER[2])
-        for jq in range(J_GROUPS):
-            for s in range(1, VIEWS):
-                normalise(jq, s)
-        quantise_w(PASS_ORDER[3])
-        for n in range(AHEAD):
-            turn(n)
-        for n in range(STEPS + LAG):
-            if n + AHEAD < STEPS:
-                turn(n + AHEAD)
-            if n < STEPS:
-                empty(n)
-            for jq, g in passes_done_at(n):
-                regroup_z(jq, g)
-            for jq, g in passes_done_at(n - 1):
-                quantise_z(jq, g)
-            if n == LAST_W_STEP:
-                for g in PASS_ORDER[EARLY_W:]:
-                    regroup_w(g, WIDE)
-                    regroup_w(g, REST)
-                    quantise_w(g)
-            for jq, g in passes_done_at(n - LAG):
-                multiply(jq, g)
+        def finish(m):
+            for acc, cols in accs[m]:
+                nc.vector.tensor_tensor(out=tok_bias[:, m, cols], in0=acc[:], in1=tok_bias[:, m, cols], op=ALU.add)
+            nc.sync.dma_start(out=token_rows(out, m), in_=tok_bias[:, m, :])
+
+        def normalise_all(engine, j):
+            for part in range(2):
+                for s in range(VIEWS):
+                    if s > 0 or part == 0:
+                        normalise(engine, j, s, (part,))
+
+        normalise_all("scalar", 3)
+        for part in range(2):
+            for j in range(3):
+                for s in range(VIEWS):
+                    if s > 0 or part == 0:
+                        normalise("vector", j, s, (part,))
+        steps = [(jq, g) for jq in range(J_GROUPS) for g in range(PASSES)]
+        for parity in range(2):
+            turn(0, 0, parity)
+        multiply_after = {3: [0], 4: [1, 2], 5: [3, 4], 7: [5], 8: [6, 7], 9: [8, 9]}
+        for n in range(len(steps)):
+            if n + 1 < len(steps):
+                for parity in range(2):
+                    turn(*steps[n + 1], parity)
+            for parity in range(2):
+                empty(*steps[n], parity)
+            regroup_z(*steps[n])
+            if n == 0:
+                normalise_all("scalar", 6)
+                normalise_all("vector", 4)
+                regroup_w("vector", 1, slice(N_WIDE // 2, N_WIDE))
+            if n == 1:
+                normalise_all("scalar", 7)
+                normalise_all("vector", 5)
+                regroup_w("vector", 2, WIDE)
+                quantise_w(1)
+            if n == 2:
+                regroup_w("scalar", 4, WIDE)
+                regroup_w("vector", 2, REST)
+                regroup_w("vector", 3, REST)
+                quantise_w(2)
+            if n == 3:
+                regroup_w("scalar", 4, REST)
+                regroup_w("vector", 3, WIDE)
+            if n == 4:
+                quantise_w(3)
+                quantise_w(4)
+            if 5 <= n < 9:
+                add_bias(n - 5)
+            if n == 6:
+                finish(0)
+                finish(1)
+            quantise_z(*steps[n])
+            for done in multiply_after.get(n, []):
+                multiply(*steps[done])
+        finish(2)
+        finish(3)

@@ -100,14 +100,14 @@ def tile_shiftedpatchtokenization_pb_kernel(tc, x, ln2_g, ln2_b, w2, b2, tok, ou
 
         rows_in = keep.tile([P, PASS_K + P], BF16)
         nc.vector.memset(rows_in[:], 0.0)
+        nc.scalar.dma_start(out=rows_in[0:PASSES, 0:PASS_K], in_=ln2_g.rearrange("(g k) -> g k", k=PASS_K))
+        nc.scalar.dma_start(out=rows_in[32 : 32 + PASSES, 0:PASS_K], in_=ln2_b.rearrange("(g k) -> g k", k=PASS_K))
+        nc.scalar.dma_start(out=rows_in[0 : DIM // P, PASS_K:], in_=b2.rearrange("(s p) -> s p", p=P))
         for c in range(CH):
             load_image(0, c)
         for c in range(CH):
             load_image(1, c)
         load_w(0)
-        nc.scalar.dma_start(out=rows_in[0:PASSES, 0:PASS_K], in_=ln2_g.rearrange("(g k) -> g k", k=PASS_K))
-        nc.scalar.dma_start(out=rows_in[32 : 32 + PASSES, 0:PASS_K], in_=ln2_b.rearrange("(g k) -> g k", k=PASS_K))
-        nc.scalar.dma_start(out=rows_in[0 : DIM // P, PASS_K:], in_=b2.rearrange("(s p) -> s p", p=P))
 
         ident = keep.tile([P, P], F32)
         make_identity(nc, ident[:])
@@ -226,13 +226,6 @@ def tile_shiftedpatchtokenization_pb_kernel(tc, x, ln2_g, ln2_b, w2, b2, tok, ou
             for i in range(GRID - 1):
                 nc.sync.dma_start(out=above[i + 1 : P : GRID, :, :, :], in_=detail[i:P:GRID, HALF_ROWS:PATCH, :, :])
 
-        rows_f32 = keep.tile([P, PACK + 1, P], F32)
-        nc.vector.tensor_copy(
-            out=rows_f32[:, 0:PACK, :].rearrange("p t (a e) -> p a t e", e=4),
-            in_=rows_in[:, 0:PASS_K].rearrange("p (a t e) -> p a t e", t=PACK, e=4),
-        )
-        nc.vector.tensor_copy(out=rows_f32[:, PACK, :], in_=rows_in[:, PASS_K:])
-
         for bank in (0, 1):
             for c in range(CH):
                 haar_taps(bank, c)
@@ -243,6 +236,12 @@ def tile_shiftedpatchtokenization_pb_kernel(tc, x, ln2_g, ln2_b, w2, b2, tok, ou
         for bank in (2, 3):
             for c in range(CH):
                 haar_taps(bank, c)
+        rows_f32 = keep.tile([P, PACK + 1, P], F32)
+        nc.vector.tensor_copy(
+            out=rows_f32[:, 0:PACK, :].rearrange("p t (a e) -> p a t e", e=4),
+            in_=rows_in[:, 0:PASS_K].rearrange("p (a t e) -> p a t e", t=PACK, e=4),
+        )
+        nc.vector.tensor_copy(out=rows_f32[:, PACK, :], in_=rows_in[:, PASS_K:])
         gain_ps = acc_psum.tile([P, PACK, P], F32, tag="wide0")
         b2_ps = acc_psum.tile([P, P], F32, tag="rest0")
         for t in range(PACK):
@@ -256,11 +255,10 @@ def tile_shiftedpatchtokenization_pb_kernel(tc, x, ln2_g, ln2_b, w2, b2, tok, ou
         haar_join(2)
         haar_join(3)
         send_above()
-        load_w(2)
-        for g in (3, 4):
-            load_w(g)
         for m in range(4):
             load_tok(m)
+        for g in (2, 3, 4):
+            load_w(g)
         strip_moments(1)
         b2_wide = acc_psum.tile([P, N_WIDE], F32, tag="wide1")
         b2_rest = acc_psum.tile([P, DIM - N_WIDE], F32, tag="rest1")
@@ -277,11 +275,10 @@ def tile_shiftedpatchtokenization_pb_kernel(tc, x, ln2_g, ln2_b, w2, b2, tok, ou
             nc.vector.tensor_tensor(out=tok_bias[:, m, :], in0=tok_in[:, m, :], in1=b2_all[:], op=ALU.add)
 
         regroup_w("scalar", 0, REST)
-        regroup_w("scalar", 0, WIDE)
+        regroup_w("scalar", 0, slice(0, N_WIDE // 2))
+        regroup_w("scalar", 0, slice(N_WIDE // 2, N_WIDE))
         nc.scalar.copy(out=b2_all[:, WIDE], in_=b2_wide[:])
         nc.scalar.copy(out=b2_all[:, REST], in_=b2_rest[:])
-        regroup_w("scalar", 1, REST)
-        regroup_w("scalar", 1, slice(0, N_WIDE // 2))
 
         stats = strip_stats[:].rearrange("p h e (o f) -> p (h e) o f", o=2)
         mean_squares = keep.tile([P, HALVES * STRIPS, 2], F32)
@@ -437,18 +434,17 @@ def tile_shiftedpatchtokenization_pb_kernel(tc, x, ln2_g, ln2_b, w2, b2, tok, ou
                 nc.vector.tensor_tensor(out=tok_bias[:, m, cols], in0=acc[:], in1=tok_bias[:, m, cols], op=ALU.add)
             nc.sync.dma_start(out=token_rows(out, m), in_=tok_bias[:, m, :])
 
-        def normalise_all(engine, j):
-            for part in range(2):
-                for s in range(VIEWS):
-                    if s > 0 or part == 0:
-                        normalise(engine, j, s, (part,))
+        def normalise_columns(engine, columns):
+            for kind in ((0, 2, 4), (1, 3)):
+                for j in columns:
+                    for s in kind:
+                        for part in range(2 if s > 0 else 1):
+                            normalise(engine, j, s, (part,))
 
-        normalise_all("scalar", 3)
-        for part in range(2):
-            for j in range(3):
-                for s in range(VIEWS):
-                    if s > 0 or part == 0:
-                        normalise("vector", j, s, (part,))
+        normalise_columns("scalar", (3,))
+        normalise_columns("vector", (0, 1, 2))
+        add_bias(0)
+        add_bias(1)
         steps = [(jq, g) for jq in range(J_GROUPS) for g in range(PASSES)]
         for parity in range(2):
             turn(0, 0, parity)
@@ -461,27 +457,30 @@ def tile_shiftedpatchtokenization_pb_kernel(tc, x, ln2_g, ln2_b, w2, b2, tok, ou
                 empty(*steps[n], parity)
             regroup_z(*steps[n])
             if n == 0:
-                normalise_all("scalar", 6)
-                normalise_all("vector", 4)
-                regroup_w("vector", 1, slice(N_WIDE // 2, N_WIDE))
+                normalise_columns("scalar", (6,))
+                normalise_columns("vector", (4, 5))
+                regroup_w("vector", 1, WIDE)
             if n == 1:
-                normalise_all("scalar", 7)
-                normalise_all("vector", 5)
+                normalise_columns("scalar", (7,))
+                regroup_w("vector", 1, REST)
                 regroup_w("vector", 2, WIDE)
                 quantise_w(1)
             if n == 2:
-                regroup_w("scalar", 4, WIDE)
+                regroup_w("scalar", 3, WIDE)
                 regroup_w("vector", 2, REST)
-                regroup_w("vector", 3, REST)
                 quantise_w(2)
             if n == 3:
-                regroup_w("scalar", 4, REST)
-                regroup_w("vector", 3, WIDE)
+                regroup_w("scalar", 3, REST)
+                regroup_w("vector", 4, WIDE)
             if n == 4:
                 quantise_w(3)
+                regroup_w("scalar", 4, REST)
+            if n == 5:
                 quantise_w(4)
-            if 5 <= n < 9:
-                add_bias(n - 5)
+            if n == 7:
+                add_bias(2)
+            if n == 8:
+                add_bias(3)
             if n == 6:
                 finish(0)
                 finish(1)

@@ -36,11 +36,11 @@ PLANE_LEN = PASSES * P
 PLANE_PITCH = 704
 UNIT = 4
 PAIR = VIEWS * UNIT
-J_GROUP = 4
-J_GROUPS = GRID // J_GROUP
 J_TILE = 2
-TILES = J_GROUP // J_TILE
-GROUP_TOKENS = BATCH * GRID * J_GROUP
+TILES = GRID // J_TILE
+TILE_TOKENS = BATCH * GRID * J_TILE
+TOKENS = TILES * TILE_TOKENS
+TILE_GROUPS = ((0, 1), (2, 3))
 N_WIDE = 512
 WIDE = slice(0, N_WIDE)
 REST = slice(N_WIDE, DIM)
@@ -70,12 +70,12 @@ def tile_shiftedpatchtokenization_pb_kernel(tc, x, ln2_g, ln2_b, w2, b2, tok, ou
         below = keep.tile([P, HALF_ROWS, PADDED_W, CH], F32)
         w_codes = keep.tile([P, PASSES, DIM], U32, align_bytes=64)
         w_scales = keep.tile([P, PASSES, DIM], U8, align_bytes=64)
-        z_codes = keep.tile([P, PASSES, J_GROUPS * GROUP_TOKENS], U32, align_bytes=64)
-        z_scales = keep.tile([P, PASSES, J_GROUPS * GROUP_TOKENS], U8, align_bytes=64)
+        z_codes = keep.tile([P, PASSES, TOKENS], U32, align_bytes=64)
+        z_scales = keep.tile([P, PASSES, TOKENS], U8, align_bytes=64)
         tok_in = keep.tile([P, 4, DIM], BF16)
         tok_bias = keep.tile([P, 4, DIM], F32)
         normed = keep.tile([P, GRID * 2 * PLANE_PITCH + 2 * PAIR], F32, align_bytes=64)
-        planes = keep.tile([P, PASSES, PACK, J_GROUPS, GROUP_TOKENS], BF16)
+        planes = keep.tile([P, PASSES, PACK, TOKENS], BF16)
 
         def token_rows(dram, m):
             return dram.rearrange("b (i q j) d -> q (b i) j d", q=4, j=J_TILE)[m]
@@ -100,14 +100,14 @@ def tile_shiftedpatchtokenization_pb_kernel(tc, x, ln2_g, ln2_b, w2, b2, tok, ou
 
         rows_in = keep.tile([P, PASS_K + P], BF16)
         nc.vector.memset(rows_in[:], 0.0)
-        nc.scalar.dma_start(out=rows_in[0:PASSES, 0:PASS_K], in_=ln2_g.rearrange("(g k) -> g k", k=PASS_K))
-        nc.scalar.dma_start(out=rows_in[32 : 32 + PASSES, 0:PASS_K], in_=ln2_b.rearrange("(g k) -> g k", k=PASS_K))
-        nc.scalar.dma_start(out=rows_in[0 : DIM // P, PASS_K:], in_=b2.rearrange("(s p) -> s p", p=P))
         for c in range(CH):
             load_image(0, c)
         for c in range(CH):
             load_image(1, c)
         load_w(0)
+        nc.sync.dma_start(out=rows_in[0:PASSES, 0:PASS_K], in_=ln2_g.rearrange("(g k) -> g k", k=PASS_K))
+        nc.sync.dma_start(out=rows_in[32 : 32 + PASSES, 0:PASS_K], in_=ln2_b.rearrange("(g k) -> g k", k=PASS_K))
+        nc.sync.dma_start(out=rows_in[0 : DIM // P, PASS_K:], in_=b2.rearrange("(s p) -> s p", p=P))
 
         ident = keep.tile([P, P], F32)
         make_identity(nc, ident[:])
@@ -115,15 +115,17 @@ def tile_shiftedpatchtokenization_pb_kernel(tc, x, ln2_g, ln2_b, w2, b2, tok, ou
         one_root = keep.tile([P, 1], F32)
         nc.gpsimd.memset(one[:], 1.0)
         nc.scalar.activation(out=one_root[:], in_=one[:], func=ACT.Sqrt)
-        strips = keep.tile([P, HALVES, 2, 18], F32)
+        sums = keep.tile([P, HALVES, 2, STRIPS + 2, 2], F32)
         nc.gpsimd.memset(detail[:, :, 0:SHIFT, :], 0.0)
         nc.gpsimd.memset(detail[:, :, SHIFT + DETAIL_W : PADDED_W, :], 0.0)
         nc.gpsimd.memset(above[:], 0.0)
         nc.gpsimd.memset(below[:], 0.0)
-        nc.gpsimd.memset(strips[:], 0.0)
+        nc.gpsimd.memset(sums[:], 0.0)
 
         neg_ident = keep.tile([P, P], BF16)
         nc.vector.tensor_scalar(out=neg_ident[:], in0=ident[:], scalar1=-1.0, scalar2=None, op0=ALU.mult)
+        ident_3 = keep.tile([P, P], BF16)
+        nc.vector.tensor_scalar(out=ident_3[:], in0=ident[:], scalar1=3.0, scalar2=None, op0=ALU.mult)
         turn_order = keep.tile([P, P], F32)
         ident_v = ident[:].rearrange("p (b h i) -> p b h i", h=CH_HALVES, i=GRID)
         nc.vector.tensor_copy(
@@ -170,43 +172,56 @@ def tile_shiftedpatchtokenization_pb_kernel(tc, x, ln2_g, ln2_b, w2, b2, tok, ou
         pixels = [t[:].rearrange("p c (r u j v) -> p c r u j v", r=HALF_ROWS, u=2, j=DETAIL_W, v=2) for t in images]
         banks = {}
 
+        TAPS = {1: ((0, 1), (1, 0), (1, 1)), 2: ((0, 0), (0, 1), (1, 0), (1, 1)), 3: ((0, 0), (0, 1), (1, 0), (1, 1))}
+
         def haar_taps(bank, c):
             if bank not in banks:
-                lower = turn_psum.tile([P, CH, BANK_ROWS, DETAIL_W], F32, tag="turned")
-                banks[bank] = lower
+                summed = turn_psum.tile([P, CH, BANK_ROWS, DETAIL_W], F32, tag="turned")
+                banks[bank] = summed
             hr, first = divmod(bank * BANK_ROWS, HALF_ROWS)
-            taps = ((1, 0), (1, 1)) if bank == 0 else ((0, 1), (1, 0), (1, 1))
-            for n, (u, v) in enumerate(taps):
+            for n, (u, v) in enumerate(TAPS[bank]):
                 nc.tensor.matmul(
                     out=banks[bank][:, c, :, :],
-                    lhsT=neg_ident[:],
+                    lhsT=neg_ident[:] if (u, v) != (0, 0) else ident_3[:],
                     rhs=pixels[hr][:, c, first : first + BANK_ROWS, u, :, v],
                     start=(n == 0),
-                    stop=(n == len(taps) - 1),
+                    stop=(n == len(TAPS[bank]) - 1),
                 )
 
-        def haar_row(row, in1, op1):
-            nc.vector.scalar_tensor_tensor(
-                out=detail[:, row, SHIFT : SHIFT + DETAIL_W, :],
-                in0=pixels[row // HALF_ROWS][:, :, row % HALF_ROWS, 0, :, 0].rearrange("p c j -> p j c"),
-                scalar=3.0,
-                in1=in1.rearrange("p c j -> p j c"),
-                op0=ALU.mult,
-                op1=op1,
-            )
+        def inside(row):
+            return detail[:, row, SHIFT : SHIFT + DETAIL_W, :]
+
+        def pixel(row, u, v):
+            return pixels[row // HALF_ROWS][:, :, row % HALF_ROWS, u, :, v].rearrange("p c j -> p j c")
+
+        def haar_vector():
+            lower = keep.tile([P, BANK_ROWS, DETAIL_W, CH], F32)
+            for row in range(BANK_ROWS):
+                nc.vector.scalar_tensor_tensor(
+                    out=inside(row), in0=pixel(row, 0, 0), scalar=3.0, in1=pixel(row, 0, 1), op0=ALU.mult, op1=ALU.subtract
+                )
+            for row in range(BANK_ROWS):
+                nc.vector.tensor_tensor(out=lower[:, row, :, :], in0=pixel(row, 1, 0), in1=pixel(row, 1, 1), op=ALU.add)
+            for row in range(BANK_ROWS):
+                nc.vector.tensor_tensor(out=inside(row), in0=inside(row), in1=lower[:, row, :, :], op=ALU.subtract)
 
         def haar_join(bank):
             for r in range(BANK_ROWS):
-                haar_row(bank * BANK_ROWS + r, banks[bank][:, :, r, :], ALU.add)
-
-        def haar_first_bank():
-            for row in range(BANK_ROWS):
-                haar_row(row, pixels[0][:, :, row, 0, :, 1], ALU.subtract)
-            for row in range(BANK_ROWS):
-                inside = detail[:, row, SHIFT : SHIFT + DETAIL_W, :]
-                nc.vector.tensor_tensor(
-                    out=inside, in0=inside, in1=banks[0][:, :, row, :].rearrange("p c j -> p j c"), op=ALU.add
+                row = bank * BANK_ROWS + r
+                nc.vector.scalar_tensor_tensor(
+                    out=inside(row),
+                    in0=pixel(row, 0, 0),
+                    scalar=3.0,
+                    in1=banks[bank][:, :, r, :].rearrange("p c j -> p j c"),
+                    op0=ALU.mult,
+                    op1=ALU.add,
                 )
+
+        def haar_copy(bank):
+            rows = slice(bank * BANK_ROWS, (bank + 1) * BANK_ROWS)
+            nc.scalar.copy(
+                out=detail[:, rows, SHIFT : SHIFT + DETAIL_W, :], in_=banks[bank][:].rearrange("p c r j -> p r j c")
+            )
 
         strip_stats = keep.tile([P, HALVES, STRIPS, 6], F32)
 
@@ -226,40 +241,99 @@ def tile_shiftedpatchtokenization_pb_kernel(tc, x, ln2_g, ln2_b, w2, b2, tok, ou
             for i in range(GRID - 1):
                 nc.sync.dma_start(out=above[i + 1 : P : GRID, :, :, :], in_=detail[i:P:GRID, HALF_ROWS:PATCH, :, :])
 
-        for bank in (0, 1):
-            for c in range(CH):
-                haar_taps(bank, c)
-        haar_first_bank()
+        warm = acc_psum.tile([P, 2, P], F32, tag="wide1")
+        for n in range(2):
+            nc.tensor.matmul(out=warm[:, n, :], lhsT=ident[:], rhs=ident[:], start=True, stop=True)
+        for c in range(CH):
+            haar_taps(1, c)
+        haar_vector()
         haar_join(1)
         send_below()
         load_w(1)
-        for bank in (2, 3):
-            for c in range(CH):
+        for c in range(CH):
+            for bank in (2, 3):
                 haar_taps(bank, c)
-        rows_f32 = keep.tile([P, PACK + 1, P], F32)
-        nc.vector.tensor_copy(
-            out=rows_f32[:, 0:PACK, :].rearrange("p t (a e) -> p a t e", e=4),
-            in_=rows_in[:, 0:PASS_K].rearrange("p (a t e) -> p a t e", t=PACK, e=4),
-        )
-        nc.vector.tensor_copy(out=rows_f32[:, PACK, :], in_=rows_in[:, PASS_K:])
-        gain_ps = acc_psum.tile([P, PACK, P], F32, tag="wide0")
-        b2_ps = acc_psum.tile([P, P], F32, tag="rest0")
-        for t in range(PACK):
-            nc.tensor.transpose(out=gain_ps[:, t, :], in_=rows_f32[:, t, :], identity=ident[:])
-        nc.tensor.transpose(out=b2_ps[:], in_=rows_f32[:, PACK, :], identity=ident[:])
-        gain_t = keep.tile([P, PACK, P], F32)
-        b2_t = keep.tile([P, DIM // P], F32)
-        nc.scalar.copy(out=b2_t[:], in_=b2_ps[:, 0 : DIM // P])
-        nc.scalar.copy(out=gain_t[:], in_=gain_ps[:])
+        haar_copy(2)
+        haar_copy(3)
+        regroup_w("scalar", 0, REST)
         strip_moments(0)
-        haar_join(2)
-        haar_join(3)
         send_above()
         for m in range(4):
             load_tok(m)
         for g in (2, 3, 4):
             load_w(g)
         strip_moments(1)
+        rows_f32 = keep.tile([P, PACK + 1, P], F32)
+        nc.scalar.copy(
+            out=rows_f32[:, 0:PACK, :].rearrange("p t (a e) -> p a t e", e=4),
+            in_=rows_in[:, 0:PASS_K].rearrange("p (a t e) -> p a t e", t=PACK, e=4),
+        )
+        nc.scalar.copy(out=rows_f32[:, PACK, :], in_=rows_in[:, PASS_K:])
+        gain_ps = acc_psum.tile([P, PACK, P], F32, tag="wide0")
+        b2_ps = acc_psum.tile([P, P], F32, tag="rest0")
+        for t in range(PACK):
+            nc.tensor.transpose(out=gain_ps[:, t, :], in_=rows_f32[:, t, :], identity=ident[:])
+        nc.tensor.transpose(out=b2_ps[:], in_=rows_f32[:, PACK, :], identity=ident[:])
+        regroup_w("scalar", 0, slice(N_WIDE // 2, N_WIDE))
+        gain_t = keep.tile([P, PACK, P], F32)
+        b2_t = keep.tile([P, DIM // P], F32)
+        nc.scalar.copy(out=b2_t[:], in_=b2_ps[:, 0 : DIM // P])
+        nc.scalar.copy(out=gain_t[:], in_=gain_ps[:])
+        b2_all = keep.tile([P, DIM], BF16)
+
+        def add_bias(m):
+            nc.vector.tensor_tensor(out=tok_bias[:, m, :], in0=tok_in[:, m, :], in1=b2_all[:], op=ALU.add)
+
+
+        def fill(n):
+            g, first = (0, 0) if n < 4 else (1, 4)
+            regroup_w("vector", g, slice(64 * (n - first), 64 * (n - first + 1)))
+
+
+        means = strip_stats[:].rearrange("p h e (o f) -> p h e o f", o=2)[:, :, :, :, 1]
+        spreads = strip_stats[:].rearrange("p h e (o f) -> p h e o f", o=2)[:, :, :, :, 2]
+        mean_squares = keep.tile([P, HALVES, STRIPS, 2], F32)
+        nc.vector.tensor_tensor(out=mean_squares[:], in0=means, in1=means, op=ALU.mult)
+        nc.vector.tensor_copy(out=sums[:, :, 0, 1 : 1 + STRIPS, :], in_=means)
+        fill(0)
+        nc.vector.scalar_tensor_tensor(
+            out=sums[:, :, 1, 1 : 1 + STRIPS, :].rearrange("p h e o -> p h (e o)"),
+            in0=mean_squares[:].rearrange("p h e o -> p (h e o)"),
+            scalar=float(STRIP_HALF),
+            in1=strip_stats[:].rearrange("p h e (o f) -> p (h e o) f", o=2)[:, :, 2],
+            op0=ALU.mult,
+            op1=ALU.add,
+        )
+        fill(1)
+        inner = keep.tile([P, HALVES * 2, GRID], F32)
+        across = keep.tile([P, HALVES * 2, GRID + 1], F32)
+        outer = keep.tile([P, HALVES * 2, GRID], F32)
+        both = keep.tile([P, HALVES * 2, GRID], F32)
+        own = keep.tile([P, 2, GRID], F32)
+        nc.vector.tensor_reduce(
+            out=across[:], in_=sums[:].rearrange("p h q (j v) o -> p (h q) j (v o)", v=2), axis=AX.X, op=ALU.add
+        )
+        nc.vector.tensor_reduce(
+            out=inner[:],
+            in_=sums[:, :, :, 1 : 1 + STRIPS, :].rearrange("p h q (j v) o -> p (h q) j (v o)", v=2),
+            axis=AX.X,
+            op=ALU.add,
+        )
+        nc.vector.tensor_tensor(out=outer[:], in0=across[:, :, 0:GRID], in1=across[:, :, 1 : GRID + 1], op=ALU.add)
+        fill(2)
+        nc.vector.tensor_tensor(out=both[:], in0=outer[:], in1=inner[:], op=ALU.add)
+        fill(3)
+        nc.vector.tensor_tensor(out=own[:], in0=both[:, 0:2, :], in1=both[:, 2:4, :], op=ALU.add)
+        moments = turn_psum.tile([P, 2, GRID], F32, tag="turned")
+        terms = ((sum_above, outer[:, 2:4, :]), (sum_below, outer[:, 0:2, :]), (sum_own, own[:]))
+        for n, (mat, part_sums) in enumerate(terms):
+            nc.tensor.matmul(
+                out=moments[:].rearrange("p q j -> p (q j)"),
+                lhsT=mat[:],
+                rhs=part_sums.rearrange("p q j -> p (q j)"),
+                start=(n == 0),
+                stop=(n == len(terms) - 1),
+            )
         b2_wide = acc_psum.tile([P, N_WIDE], F32, tag="wide1")
         b2_rest = acc_psum.tile([P, DIM - N_WIDE], F32, tag="rest1")
         for s in range(DIM // P):
@@ -268,55 +342,6 @@ def tile_shiftedpatchtokenization_pb_kernel(tc, x, ln2_g, ln2_b, w2, b2, tok, ou
                 out=bank[:, (s - first) * P : (s - first + 1) * P],
                 in_=b2_t[:, s : s + 1].to_broadcast([P, P]),
                 identity=ident[:],
-            )
-        b2_all = keep.tile([P, DIM], BF16)
-
-        def add_bias(m):
-            nc.vector.tensor_tensor(out=tok_bias[:, m, :], in0=tok_in[:, m, :], in1=b2_all[:], op=ALU.add)
-
-        regroup_w("scalar", 0, REST)
-        regroup_w("scalar", 0, slice(0, N_WIDE // 2))
-        regroup_w("scalar", 0, slice(N_WIDE // 2, N_WIDE))
-        nc.scalar.copy(out=b2_all[:, WIDE], in_=b2_wide[:])
-        nc.scalar.copy(out=b2_all[:, REST], in_=b2_rest[:])
-
-        stats = strip_stats[:].rearrange("p h e (o f) -> p (h e) o f", o=2)
-        mean_squares = keep.tile([P, HALVES * STRIPS, 2], F32)
-        square_sums = keep.tile([P, HALVES * STRIPS, 2], F32)
-        nc.vector.tensor_tensor(out=mean_squares[:], in0=stats[:, :, :, 1], in1=stats[:, :, :, 1], op=ALU.mult)
-        nc.vector.tensor_tensor(
-            out=strips[:, :, 0, 1 : 1 + STRIPS],
-            in0=strip_stats[:, :, :, 1],
-            in1=strip_stats[:, :, :, 4],
-            op=ALU.add,
-        )
-        nc.vector.scalar_tensor_tensor(
-            out=square_sums[:], in0=mean_squares[:], scalar=float(STRIP_HALF), in1=stats[:, :, :, 2], op0=ALU.mult, op1=ALU.add
-        )
-        pairs = square_sums[:].rearrange("p (h e) o -> p h e o", h=HALVES)
-        nc.vector.tensor_tensor(out=strips[:, :, 1, 1 : 1 + STRIPS], in0=pairs[:, :, :, 0], in1=pairs[:, :, :, 1], op=ALU.add)
-        inner = keep.tile([P, HALVES, 2, GRID], F32)
-        sides = keep.tile([P, HALVES, 2, GRID], F32)
-        mid = strips[:, :, :, 1:17].rearrange("p h q (j v) -> p h q j v", v=2)
-        left = strips[:, :, :, 0:16].rearrange("p h q (j v) -> p h q j v", v=2)
-        right = strips[:, :, :, 2:18].rearrange("p h q (j v) -> p h q j v", v=2)
-        nc.vector.tensor_tensor(out=inner[:], in0=mid[:, :, :, :, 0], in1=mid[:, :, :, :, 1], op=ALU.add)
-        nc.vector.tensor_tensor(out=sides[:], in0=left[:, :, :, :, 0], in1=right[:, :, :, :, 1], op=ALU.add)
-        outer = keep.tile([P, HALVES, 2, GRID], F32)
-        both = keep.tile([P, HALVES, 2, GRID], F32)
-        own = keep.tile([P, 2, GRID], F32)
-        nc.vector.tensor_tensor(out=outer[:], in0=sides[:], in1=inner[:], op=ALU.add)
-        nc.vector.tensor_tensor(out=both[:], in0=outer[:], in1=inner[:], op=ALU.add)
-        nc.vector.tensor_tensor(out=own[:], in0=both[:, 0, :, :], in1=both[:, 1, :, :], op=ALU.add)
-        moments = turn_psum.tile([P, 2, GRID], F32, tag="turned")
-        terms = ((sum_above, outer[:, 1, :, :]), (sum_below, outer[:, 0, :, :]), (sum_own, own[:]))
-        for n, (mat, sums) in enumerate(terms):
-            nc.tensor.matmul(
-                out=moments[:].rearrange("p q j -> p (q j)"),
-                lhsT=mat[:],
-                rhs=sums.rearrange("p q j -> p (q j)"),
-                start=(n == 0),
-                stop=(n == len(terms) - 1),
             )
         quantise_w(0)
         mean = keep.tile([P, GRID], F32)
@@ -331,6 +356,9 @@ def tile_shiftedpatchtokenization_pb_kernel(tc, x, ln2_g, ln2_b, w2, b2, tok, ou
             out=var[:], in0=moments[:, 1, :], scalar=EPS, in1=mean_sq[:], op0=ALU.add, op1=ALU.subtract
         )
         nc.scalar.activation(out=std[:], in_=var[:], func=ACT.Sqrt)
+        nc.scalar.copy(out=b2_all[:, WIDE], in_=b2_wide[:])
+        fill(4)
+        fill(5)
         nc.vector.reciprocal(out=rstd[:], in_=std[:])
         nc.vector.scalar_tensor_tensor(out=shift[:], in0=mean[:], scalar=-1.0, in1=rstd[:], op0=ALU.mult, op1=ALU.mult)
 
@@ -371,52 +399,65 @@ def tile_shiftedpatchtokenization_pb_kernel(tc, x, ln2_g, ln2_b, w2, b2, tok, ou
 
         turned_tiles = {}
 
-        def turn(jq, g, parity):
-            turned = turn_psum.tile([P, J_GROUP, P], F32)
-            turned_tiles[(jq, g, parity)] = turned
-            for j4 in range(J_GROUP):
-                first = PLANE_PITCH * (2 * (jq * J_GROUP + j4) + parity) + P * g
-                nc.tensor.transpose(out=turned[:, j4, :], in_=normed[:, first : first + P], identity=turn_order[:])
+        def turn(grp, g):
+            columns = [J_TILE * m + j for m in TILE_GROUPS[grp] for j in range(J_TILE)]
+            pairs = [(parity, j) for parity in range(2) for j in columns]
+            for first in range(0, len(pairs), 4):
+                turned = turn_psum.tile([P, 4, P], F32)
+                turned_tiles[(grp, g, first // 4)] = turned
+                for n, (parity, j) in enumerate(pairs[first : first + 4]):
+                    at = PLANE_PITCH * (2 * j + parity) + P * g
+                    nc.tensor.transpose(out=turned[:, n, :], in_=normed[:, at : at + P], identity=turn_order[:])
 
-        def empty(jq, g, parity):
-            turned = turned_tiles[(jq, g, parity)][:].rearrange("p (m j) (h r) -> p h m r j", j=J_TILE, h=CH_HALVES)
-            for h in range(CH_HALVES):
-                t = 2 * parity + h
-                nc.scalar.activation(
-                    out=planes[:, g, t, jq, :].rearrange("p (m r j) -> p m r j", m=TILES, j=J_TILE),
-                    in_=turned[:, h, :, :, :],
-                    func=ACT.Identity,
-                    scale=gain_t[:, t, g : g + 1],
-                    bias=gain_t[:, t, 32 + g : 33 + g],
-                )
+        def tokens(grp):
+            tiles = TILE_GROUPS[grp]
+            return slice(TILE_TOKENS * tiles[0], TILE_TOKENS * (tiles[-1] + 1))
+
+        def empty(grp, g):
+            count = len(TILE_GROUPS[grp])
+            for parity in range(2):
+                bank, first = divmod(parity * count * J_TILE, 4)
+                turned = turned_tiles[(grp, g, bank)][:, first : first + count * J_TILE, :]
+                turned = turned.rearrange("p (m j) (h r) -> p h m r j", j=J_TILE, h=CH_HALVES)
+                for h in range(CH_HALVES):
+                    t = 2 * parity + h
+                    nc.scalar.activation(
+                        out=planes[:, g, t, tokens(grp)].rearrange("p (m r j) -> p m r j", m=count, j=J_TILE),
+                        in_=turned[:, h, :, :, :],
+                        func=ACT.Identity,
+                        scale=gain_t[:, t, g : g + 1],
+                        bias=gain_t[:, t, 32 + g : 33 + g],
+                    )
 
         z_grps = {}
 
-        def regroup_z(jq, g):
-            z_grp = z_grp_pool.tile([P, GROUP_TOKENS, PACK], BF16, align_bytes=64)
-            z_grps[(jq, g)] = z_grp
-            nc.vector.tensor_copy(
-                out=z_grp[:].rearrange("p (w i) t -> p w t i", i=4),
-                in_=planes[:, g, :, jq, :].rearrange("p t (w i) -> p w t i", i=4),
-            )
+        def regroup_z(grp, g, engine="vector"):
+            count = len(TILE_GROUPS[grp]) * TILE_TOKENS
+            z_grp = z_grp_pool.tile([P, 2 * TILE_TOKENS, PACK], BF16, align_bytes=64)
+            z_grps[(grp, g)] = z_grp
+            grouped = z_grp[:, 0:count, :].rearrange("p (w i) t -> p w t i", i=4)
+            rows = planes[:, g, :, tokens(grp)].rearrange("p t (w i) -> p w t i", i=4)
+            if engine == "scalar":
+                nc.scalar.copy(out=grouped, in_=rows)
+            else:
+                nc.vector.tensor_copy(out=grouped, in_=rows)
 
-        def quantise_z(jq, g):
-            toks = slice(jq * GROUP_TOKENS, (jq + 1) * GROUP_TOKENS)
+        def quantise_z(grp, g):
+            count = len(TILE_GROUPS[grp]) * TILE_TOKENS
             nc.vector.quantize_mx(
-                out=z_codes[:, g, toks].bitcast(FP8X4),
-                scales=z_scales[:, g, toks],
-                in_=z_grps[(jq, g)][:].rearrange("p w t -> p (w t)"),
+                out=z_codes[:, g, tokens(grp)].bitcast(FP8X4),
+                scales=z_scales[:, g, tokens(grp)],
+                in_=z_grps[(grp, g)][:, 0:count, :].rearrange("p w t -> p (w t)"),
             )
 
         accs = {}
 
-        def multiply(jq, g):
-            for tile in range(TILES):
-                m = TILES * jq + tile
+        def multiply(grp, g):
+            for m in TILE_GROUPS[grp]:
                 rows = slice(m * P, (m + 1) * P)
                 if g == 0:
-                    acc_wide = acc_psum.tile([P, N_WIDE], F32, tag="wide%d" % tile)
-                    acc_rest = acc_psum.tile([P, DIM - N_WIDE], F32, tag="rest%d" % tile)
+                    acc_wide = acc_psum.tile([P, N_WIDE], F32, tag="wide%d" % (m % 2))
+                    acc_rest = acc_psum.tile([P, DIM - N_WIDE], F32, tag="rest%d" % (m % 2))
                     accs[m] = ((acc_wide, WIDE), (acc_rest, REST))
                 for acc, cols in accs[m]:
                     nc.tensor.matmul_mx(
@@ -432,7 +473,7 @@ def tile_shiftedpatchtokenization_pb_kernel(tc, x, ln2_g, ln2_b, w2, b2, tok, ou
         def finish(m):
             for acc, cols in accs[m]:
                 nc.vector.tensor_tensor(out=tok_bias[:, m, cols], in0=acc[:], in1=tok_bias[:, m, cols], op=ALU.add)
-            nc.sync.dma_start(out=token_rows(out, m), in_=tok_bias[:, m, :])
+                nc.sync.dma_start(out=token_rows(out, m)[:, :, cols], in_=tok_bias[:, m, cols])
 
         def normalise_columns(engine, columns):
             for kind in ((0, 2, 4), (1, 3)):
@@ -441,50 +482,48 @@ def tile_shiftedpatchtokenization_pb_kernel(tc, x, ln2_g, ln2_b, w2, b2, tok, ou
                         for part in range(2 if s > 0 else 1):
                             normalise(engine, j, s, (part,))
 
+        steps = [(grp, g) for grp in range(len(TILE_GROUPS)) for g in range(PASSES)]
         normalise_columns("scalar", (3,))
-        normalise_columns("vector", (0, 1, 2))
+        nc.scalar.copy(out=b2_all[:, REST], in_=b2_rest[:])
+        regroup_w("scalar", 1, REST)
+        normalise_columns("vector", (0, 1, 2,))
         add_bias(0)
         add_bias(1)
-        steps = [(jq, g) for jq in range(J_GROUPS) for g in range(PASSES)]
-        for parity in range(2):
-            turn(0, 0, parity)
-        multiply_after = {3: [0], 4: [1, 2], 5: [3, 4], 7: [5], 8: [6, 7], 9: [8, 9]}
+        multiply_after = {3: [0], 4: [1], 5: [2], 6: [3, 4], 8: [5, 6], 9: [7, 8, 9]}
+        turn(*steps[0])
+        turn(*steps[1])
         for n in range(len(steps)):
-            if n + 1 < len(steps):
-                for parity in range(2):
-                    turn(*steps[n + 1], parity)
-            for parity in range(2):
-                empty(*steps[n], parity)
+            empty(*steps[n])
             regroup_z(*steps[n])
             if n == 0:
                 normalise_columns("scalar", (6,))
-                normalise_columns("vector", (4, 5))
-                regroup_w("vector", 1, WIDE)
+                normalise_columns("vector", (4, 5,))
+                regroup_w("vector", 1, slice(128, N_WIDE))
             if n == 1:
                 normalise_columns("scalar", (7,))
-                regroup_w("vector", 1, REST)
                 regroup_w("vector", 2, WIDE)
                 quantise_w(1)
             if n == 2:
                 regroup_w("scalar", 3, WIDE)
                 regroup_w("vector", 2, REST)
-                quantise_w(2)
+                add_bias(2)
             if n == 3:
+                quantise_w(2)
                 regroup_w("scalar", 3, REST)
                 regroup_w("vector", 4, WIDE)
             if n == 4:
-                quantise_w(3)
                 regroup_w("scalar", 4, REST)
+                quantise_w(3)
             if n == 5:
                 quantise_w(4)
-            if n == 7:
-                add_bias(2)
-            if n == 8:
-                add_bias(3)
             if n == 6:
+                add_bias(3)
+            if n == 7:
                 finish(0)
                 finish(1)
             quantise_z(*steps[n])
+            if n + 2 < len(steps):
+                turn(*steps[n + 2])
             for done in multiply_after.get(n, []):
                 multiply(*steps[done])
         finish(2)

@@ -105,9 +105,6 @@ def tile_shiftedpatchtokenization_pb_kernel(tc, x, ln2_g, ln2_b, w2, b2, tok, ou
         for c in range(CH):
             load_image(1, c)
         load_w(0)
-        nc.sync.dma_start(out=rows_in[0:PASSES, 0:PASS_K], in_=ln2_g.rearrange("(g k) -> g k", k=PASS_K))
-        nc.sync.dma_start(out=rows_in[32 : 32 + PASSES, 0:PASS_K], in_=ln2_b.rearrange("(g k) -> g k", k=PASS_K))
-        nc.sync.dma_start(out=rows_in[0 : DIM // P, PASS_K:], in_=b2.rearrange("(s p) -> s p", p=P))
 
         ident = keep.tile([P, P], F32)
         make_identity(nc, ident[:])
@@ -116,6 +113,9 @@ def tile_shiftedpatchtokenization_pb_kernel(tc, x, ln2_g, ln2_b, w2, b2, tok, ou
         nc.gpsimd.memset(one[:], 1.0)
         nc.scalar.activation(out=one_root[:], in_=one[:], func=ACT.Sqrt)
         sums = keep.tile([P, HALVES, 2, STRIPS + 2, 2], F32)
+        nc.gpsimd.dma_start(out=rows_in[0:PASSES, 0:PASS_K], in_=ln2_g.rearrange("(g k) -> g k", k=PASS_K))
+        nc.gpsimd.dma_start(out=rows_in[32 : 32 + PASSES, 0:PASS_K], in_=ln2_b.rearrange("(g k) -> g k", k=PASS_K))
+        nc.gpsimd.dma_start(out=rows_in[0 : DIM // P, PASS_K:], in_=b2.rearrange("(s p) -> s p", p=P))
         nc.gpsimd.memset(detail[:, :, 0:SHIFT, :], 0.0)
         nc.gpsimd.memset(detail[:, :, SHIFT + DETAIL_W : PADDED_W, :], 0.0)
         nc.gpsimd.memset(above[:], 0.0)

@@ -113,14 +113,14 @@ def tile_shiftedpatchtokenization_pb_kernel(tc, x, ln2_g, ln2_b, w2, b2, tok, ou
         nc.gpsimd.memset(one[:], 1.0)
         nc.scalar.activation(out=one_root[:], in_=one[:], func=ACT.Sqrt)
         sums = keep.tile([P, HALVES, 2, STRIPS + 2, 2], F32)
-        nc.gpsimd.dma_start(out=rows_in[0:PASSES, 0:PASS_K], in_=ln2_g.rearrange("(g k) -> g k", k=PASS_K))
-        nc.gpsimd.dma_start(out=rows_in[32 : 32 + PASSES, 0:PASS_K], in_=ln2_b.rearrange("(g k) -> g k", k=PASS_K))
-        nc.gpsimd.dma_start(out=rows_in[0 : DIM // P, PASS_K:], in_=b2.rearrange("(s p) -> s p", p=P))
         nc.gpsimd.memset(detail[:, :, 0:SHIFT, :], 0.0)
         nc.gpsimd.memset(detail[:, :, SHIFT + DETAIL_W : PADDED_W, :], 0.0)
         nc.gpsimd.memset(above[:], 0.0)
         nc.gpsimd.memset(below[:], 0.0)
         nc.gpsimd.memset(sums[:], 0.0)
+        nc.gpsimd.dma_start(out=rows_in[0:PASSES, 0:PASS_K], in_=ln2_g.rearrange("(g k) -> g k", k=PASS_K))
+        nc.gpsimd.dma_start(out=rows_in[32 : 32 + PASSES, 0:PASS_K], in_=ln2_b.rearrange("(g k) -> g k", k=PASS_K))
+        nc.gpsimd.dma_start(out=rows_in[0 : DIM // P, PASS_K:], in_=b2.rearrange("(s p) -> s p", p=P))
 
         neg_ident = keep.tile([P, P], BF16)
         nc.vector.tensor_scalar(out=neg_ident[:], in0=ident[:], scalar1=-1.0, scalar2=None, op0=ALU.mult)
@@ -258,10 +258,11 @@ def tile_shiftedpatchtokenization_pb_kernel(tc, x, ln2_g, ln2_b, w2, b2, tok, ou
         regroup_w("scalar", 0, REST)
         strip_moments(0)
         send_above()
+        load_w(2)
+        load_w(3)
         for m in range(4):
             load_tok(m)
-        for g in (2, 3, 4):
-            load_w(g)
+        load_w(4)
         strip_moments(1)
         rows_f32 = keep.tile([P, PACK + 1, P], F32)
         nc.scalar.copy(
@@ -487,8 +488,8 @@ def tile_shiftedpatchtokenization_pb_kernel(tc, x, ln2_g, ln2_b, w2, b2, tok, ou
         nc.scalar.copy(out=b2_all[:, REST], in_=b2_rest[:])
         regroup_w("scalar", 1, REST)
         normalise_columns("vector", (0, 1, 2,))
-        add_bias(0)
-        add_bias(1)
+        regroup_w("vector", 1, slice(128, N_WIDE))
+        quantise_w(1)
         multiply_after = {3: [0], 4: [1], 5: [2], 6: [3, 4], 8: [5, 6], 9: [7, 8, 9]}
         turn(*steps[0])
         turn(*steps[1])
@@ -498,18 +499,18 @@ def tile_shiftedpatchtokenization_pb_kernel(tc, x, ln2_g, ln2_b, w2, b2, tok, ou
             if n == 0:
                 normalise_columns("scalar", (6,))
                 normalise_columns("vector", (4, 5,))
-                regroup_w("vector", 1, slice(128, N_WIDE))
+                regroup_w("vector", 2, slice(0, 256))
             if n == 1:
                 normalise_columns("scalar", (7,))
-                regroup_w("vector", 2, WIDE)
-                quantise_w(1)
+                regroup_w("vector", 2, slice(256, N_WIDE))
+                regroup_w("vector", 2, REST)
             if n == 2:
                 regroup_w("scalar", 3, WIDE)
-                regroup_w("vector", 2, REST)
-                add_bias(2)
-            if n == 3:
                 quantise_w(2)
+                add_bias(0)
+            if n == 3:
                 regroup_w("scalar", 3, REST)
+                add_bias(1)
                 regroup_w("vector", 4, WIDE)
             if n == 4:
                 regroup_w("scalar", 4, REST)
@@ -517,10 +518,12 @@ def tile_shiftedpatchtokenization_pb_kernel(tc, x, ln2_g, ln2_b, w2, b2, tok, ou
             if n == 5:
                 quantise_w(4)
             if n == 6:
-                add_bias(3)
+                add_bias(2)
             if n == 7:
                 finish(0)
                 finish(1)
+            if n == 8:
+                add_bias(3)
             quantise_z(*steps[n])
             if n + 2 < len(steps):
                 turn(*steps[n + 2])

@@ -490,31 +490,30 @@ def tile_shiftedpatchtokenization_pb_kernel(tc, x, ln2_g, ln2_b, w2, b2, tok, ou
         normalise_columns("vector", (0, 1, 2,))
         regroup_w("vector", 1, slice(128, N_WIDE))
         quantise_w(1)
-        multiply_after = {3: [0], 4: [1], 5: [2], 6: [3, 4], 8: [5, 6], 9: [7, 8, 9]}
+        multiply_after = {2: [0], 3: [1], 4: [2], 5: [3], 6: [4], 7: [5, 6], 8: [7], 9: [8, 9]}
         turn(*steps[0])
         turn(*steps[1])
         for n in range(len(steps)):
             empty(*steps[n])
-            regroup_z(*steps[n])
+            regroup_z(*steps[n], "scalar" if n in (3, 6, 9) else "vector")
             if n == 0:
-                normalise_columns("scalar", (6,))
                 normalise_columns("vector", (4, 5,))
-                regroup_w("vector", 2, slice(0, 256))
             if n == 1:
                 normalise_columns("scalar", (7,))
-                regroup_w("vector", 2, slice(256, N_WIDE))
-                regroup_w("vector", 2, REST)
+                normalise_columns("vector", (6,))
+                regroup_w("vector", 2, WIDE)
+                regroup_w("scalar", 2, REST)
             if n == 2:
-                regroup_w("scalar", 3, WIDE)
                 quantise_w(2)
-                add_bias(0)
-            if n == 3:
+                regroup_w("vector", 3, WIDE)
                 regroup_w("scalar", 3, REST)
-                add_bias(1)
-                regroup_w("vector", 4, WIDE)
-            if n == 4:
-                regroup_w("scalar", 4, REST)
+            if n == 3:
                 quantise_w(3)
+                add_bias(0)
+            if n == 4:
+                regroup_w("vector", 4, WIDE)
+                regroup_w("scalar", 4, REST)
+                add_bias(1)
             if n == 5:
                 quantise_w(4)
             if n == 6:

@@ -241,11 +241,17 @@ def tile_shiftedpatchtokenization_pb_kernel(tc, x, ln2_g, ln2_b, w2, b2, tok, ou
             for i in range(GRID - 1):
                 nc.sync.dma_start(out=above[i + 1 : P : GRID, :, :, :], in_=detail[i:P:GRID, HALF_ROWS:PATCH, :, :])
 
-        warm = acc_psum.tile([P, 2, P], F32, tag="wide1")
-        for n in range(2):
-            nc.tensor.matmul(out=warm[:, n, :], lhsT=ident[:], rhs=ident[:], start=True, stop=True)
+        warm = acc_psum.tile([P, P], F32, tag="wide1")
+
+        def keep_clock(columns):
+            nc.tensor.matmul(out=warm[:, 0:columns], lhsT=ident[:], rhs=ident[:, 0:columns], start=True, stop=True)
+
+        keep_clock(P)
+        keep_clock(P)
         for c in range(CH):
             haar_taps(1, c)
+            if c < CH - 1:
+                keep_clock(P // 2)
         haar_vector()
         haar_join(1)
         send_below()
@@ -521,12 +527,11 @@ def tile_shiftedpatchtokenization_pb_kernel(tc, x, ln2_g, ln2_b, w2, b2, tok, ou
             if n == 7:
                 finish(0)
                 finish(1)
-            if n == 8:
-                add_bias(3)
             quantise_z(*steps[n])
             if n + 2 < len(steps):
                 turn(*steps[n + 2])
             for done in multiply_after.get(n, []):
                 multiply(*steps[done])
+        add_bias(3)
         finish(2)
         finish(3)

from contextlib import ExitStack

import concourse.mybir as mybir
from concourse.masks import make_identity

F32 = mybir.dt.float32
BF16 = mybir.dt.bfloat16
U32 = mybir.dt.uint32
U8 = mybir.dt.uint8
FP8X4 = mybir.dt.float8_e4m3fn_x4
ALU = mybir.AluOpType
ACT = mybir.ActivationFunctionType
AX = mybir.AxisListType

P = 128
BATCH = 8
CH_HALVES = 2
CH = 4
GROUPS = BATCH * CH_HALVES
GRID = 8
PATCH = 8
VIEWS = 5
SHIFT = 4
DETAIL_W = 64
PADDED_W = DETAIL_W + 2 * SHIFT
ROW_PIX = 128
HALVES = 2
HALF_ROWS = 4
BANK_ROWS = 2
K = PATCH * PATCH * VIEWS * CH * CH_HALVES
DIM = 768
PACK = 4
PASS_K = P * PACK
PASSES = K // PASS_K
PLANE_LEN = PASSES * P
PLANE_PITCH = 704
UNIT = 4
PAIR = VIEWS * UNIT
J_TILE = 2
TILES = GRID // J_TILE
TILE_TOKENS = BATCH * GRID * J_TILE
TOKENS = TILES * TILE_TOKENS
TILE_GROUPS = ((0, 1), (2, 3))
N_WIDE = 512
WIDE = slice(0, N_WIDE)
REST = slice(N_WIDE, DIM)
TURN_BANKS = 4
HAAR_SCALE = 6.0
EPS = 1e-5 * HAAR_SCALE * HAAR_SCALE
STRIPS = DETAIL_W // SHIFT
STRIP_HALF = HALF_ROWS * SHIFT * CH // 2

FLOPS = 2 * BATCH * GRID * GRID * K * DIM


def tile_shiftedpatchtokenization_pb_kernel(tc, x, ln2_g, ln2_b, w2, b2, tok, out):
    nc = tc.nc
    with ExitStack() as ctx:
        keep = ctx.enter_context(tc.tile_pool(name="keep", bufs=1))
        w_raw_pool = ctx.enter_context(tc.tile_pool(name="w_raw", bufs=PASSES))
        w_grp_pool = ctx.enter_context(tc.tile_pool(name="w_grp", bufs=3))
        z_grp_pool = ctx.enter_context(tc.tile_pool(name="z_grp", bufs=3))
        turn_psum = ctx.enter_context(tc.psum_pool(name="turn_psum", bufs=TURN_BANKS))
        acc_psum = ctx.enter_context(tc.psum_pool(name="acc_psum", bufs=1))
        ctx.enter_context(tc.manual_schedule())

        images = [keep.tile([P, CH, HALF_ROWS * 2 * ROW_PIX], BF16, name="image%d" % hr) for hr in range(HALVES)]
        detail = keep.tile([P, PATCH, PADDED_W, CH], F32)
        above = keep.tile([P, HALF_ROWS, PADDED_W, CH], F32)
        below = keep.tile([P, HALF_ROWS, PADDED_W, CH], F32)
        w_codes = keep.tile([P, PASSES, DIM], U32, align_bytes=64)
        w_scales = keep.tile([P, PASSES, DIM], U8, align_bytes=64)
        z_codes = keep.tile([P, PASSES, TOKENS], U32, align_bytes=64)
        z_scales = keep.tile([P, PASSES, TOKENS], U8, align_bytes=64)
        tok_in = keep.tile([P, 4, DIM], BF16)
        tok_bias = keep.tile([P, 4, DIM], F32)
        normed = keep.tile([P, GRID * 2 * PLANE_PITCH + 2 * PAIR], F32, align_bytes=64)
        planes = keep.tile([P, PASSES, PACK, TOKENS], BF16)

        def token_rows(dram, m):
            return dram.rearrange("b (i q j) d -> q (b i) j d", q=4, j=J_TILE)[m]

        x_parts = x.rearrange("b (h c) (i r) w -> c (b h) i (r w)", h=CH_HALVES, i=GRID)
        w_parts = w2.rearrange("(g a t e) n -> g t a e n", g=PASSES, t=PACK, e=4)
        half_pix = HALF_ROWS * 2 * ROW_PIX
        w_raws = {}

        def load_image(hr, c):
            pix = slice(hr * half_pix, (hr + 1) * half_pix)
            nc.sync.dma_start(out=images[hr][:, c, :], in_=x_parts[c][:, :, pix])

        def load_w(g):
            w_raw = w_raw_pool.tile([P, PACK, DIM], BF16)
            w_raws[g] = w_raw
            for t in range(PACK):
                nc.sync.dma_start(out=w_raw[:, t, :], in_=w_parts[g][t])

        def load_tok(m):
            nc.sync.dma_start(out=tok_in[:, m, :], in_=token_rows(tok, m))

        rows_in = keep.tile([P, PASS_K + P], BF16)
        nc.vector.memset(rows_in[:], 0.0)
        for c in range(CH):
            load_image(0, c)
        for c in range(CH):
            load_image(1, c)
        load_w(0)

        ident = keep.tile([P, P], F32)
        make_identity(nc, ident[:])
        one = keep.tile([P, 1], F32)
        one_root = keep.tile([P, 1], F32)
        nc.gpsimd.memset(one[:], 1.0)
        nc.scalar.activation(out=one_root[:], in_=one[:], func=ACT.Sqrt)
        sums = keep.tile([P, HALVES, 2, STRIPS + 2, 2], F32)
        nc.gpsimd.memset(detail[:, :, 0:SHIFT, :], 0.0)
        nc.gpsimd.memset(detail[:, :, SHIFT + DETAIL_W : PADDED_W, :], 0.0)
        nc.gpsimd.memset(above[:], 0.0)
        nc.gpsimd.memset(below[:], 0.0)
        nc.gpsimd.memset(sums[:], 0.0)
        nc.gpsimd.dma_start(out=rows_in[0:PASSES, 0:PASS_K], in_=ln2_g.rearrange("(g k) -> g k", k=PASS_K))
        nc.gpsimd.dma_start(out=rows_in[32 : 32 + PASSES, 0:PASS_K], in_=ln2_b.rearrange("(g k) -> g k", k=PASS_K))
        nc.gpsimd.dma_start(out=rows_in[0 : DIM // P, PASS_K:], in_=b2.rearrange("(s p) -> s p", p=P))

        neg_ident = keep.tile([P, P], BF16)
        nc.vector.tensor_scalar(out=neg_ident[:], in0=ident[:], scalar1=-1.0, scalar2=None, op0=ALU.mult)
        ident_3 = keep.tile([P, P], BF16)
        nc.vector.tensor_scalar(out=ident_3[:], in0=ident[:], scalar1=3.0, scalar2=None, op0=ALU.mult)
        turn_order = keep.tile([P, P], F32)
        ident_v = ident[:].rearrange("p (b h i) -> p b h i", h=CH_HALVES, i=GRID)
        nc.vector.tensor_copy(
            out=turn_order[:].rearrange("p (h b i) -> p b h i", h=CH_HALVES, i=GRID),
            in_=ident_v,
        )
        row_sum = keep.tile([P, BATCH, GRID + 2], F32)
        nc.vector.memset(row_sum[:], 0.0)
        nc.vector.tensor_tensor(out=row_sum[:, :, 1 : GRID + 1], in0=ident_v[:, :, 0, :], in1=ident_v[:, :, 1, :], op=ALU.add)
        nc.vector.tensor_scalar(
            out=row_sum[:, :, 1 : GRID + 1], in0=row_sum[:, :, 1 : GRID + 1], scalar1=1.0 / K, scalar2=None, op0=ALU.mult
        )
        sum_mats = []
        for name, first in (("own", 1), ("above", 0), ("below", 2)):
            mat = keep.tile([P, P], F32, name="sum_%s" % name)
            nc.vector.tensor_copy(
                out=mat[:].rearrange("p (b h i) -> p b h i", h=CH_HALVES, i=GRID),
                in_=row_sum[:, :, first : first + GRID].unsqueeze(2).to_broadcast([P, BATCH, CH_HALVES, GRID]),
            )
            sum_mats.append(mat)
        sum_own, sum_above, sum_below = sum_mats

        w_grps = {}

        def regroup_w(engine, g, cols):
            if g not in w_grps:
                w_grp = w_grp_pool.tile([P, DIM, PACK], BF16, align_bytes=64)
                w_grps[g] = w_grp
            grouped = w_grps[g][:, cols, :].rearrange("p (n i) t -> p n t i", i=4)
            rows = w_raws[g][:, :, cols].rearrange("p t (n i) -> p n t i", i=4)
            if engine == "scalar":
                nc.scalar.copy(out=grouped, in_=rows)
            else:
                nc.vector.tensor_copy(out=grouped, in_=rows)

        def quantise_w(g):
            for cols in (WIDE, REST):
                nc.vector.quantize_mx(
                    out=w_codes[:, g, cols].bitcast(FP8X4),
                    scales=w_scales[:, g, cols],
                    in_=w_grps[g][:, cols, :].rearrange("p n t -> p (n t)"),
                )

        pixels = [t[:].rearrange("p c (r u j v) -> p c r u j v", r=HALF_ROWS, u=2, j=DETAIL_W, v=2) for t in images]
        banks = {}

        TAPS = {1: ((0, 1), (1, 0), (1, 1)), 2: ((0, 0), (0, 1), (1, 0), (1, 1)), 3: ((0, 0), (0, 1), (1, 0), (1, 1))}

        def haar_taps(bank, c):
            if bank not in banks:
                summed = turn_psum.tile([P, CH, BANK_ROWS, DETAIL_W], F32, tag="turned")
                banks[bank] = summed
            hr, first = divmod(bank * BANK_ROWS, HALF_ROWS)
            for n, (u, v) in enumerate(TAPS[bank]):
                nc.tensor.matmul(
                    out=banks[bank][:, c, :, :],
                    lhsT=neg_ident[:] if (u, v) != (0, 0) else ident_3[:],
                    rhs=pixels[hr][:, c, first : first + BANK_ROWS, u, :, v],
                    start=(n == 0),
                    stop=(n == len(TAPS[bank]) - 1),
                )

        def inside(row):
            return detail[:, row, SHIFT : SHIFT + DETAIL_W, :]

        def pixel(row, u, v):
            return pixels[row // HALF_ROWS][:, :, row % HALF_ROWS, u, :, v].rearrange("p c j -> p j c")

        def haar_vector():
            lower = keep.tile([P, BANK_ROWS, DETAIL_W, CH], F32)
            for row in range(BANK_ROWS):
                nc.vector.scalar_tensor_tensor(
                    out=inside(row), in0=pixel(row, 0, 0), scalar=3.0, in1=pixel(row, 0, 1), op0=ALU.mult, op1=ALU.subtract
                )
            for row in range(BANK_ROWS):
                nc.vector.tensor_tensor(out=lower[:, row, :, :], in0=pixel(row, 1, 0), in1=pixel(row, 1, 1), op=ALU.add)
            for row in range(BANK_ROWS):
                nc.vector.tensor_tensor(out=inside(row), in0=inside(row), in1=lower[:, row, :, :], op=ALU.subtract)

        def haar_join(bank):
            for r in range(BANK_ROWS):
                row = bank * BANK_ROWS + r
                nc.vector.scalar_tensor_tensor(
                    out=inside(row),
                    in0=pixel(row, 0, 0),
                    scalar=3.0,
                    in1=banks[bank][:, :, r, :].rearrange("p c j -> p j c"),
                    op0=ALU.mult,
                    op1=ALU.add,
                )

        def haar_copy(bank):
            rows = slice(bank * BANK_ROWS, (bank + 1) * BANK_ROWS)
            nc.scalar.copy(
                out=detail[:, rows, SHIFT : SHIFT + DETAIL_W, :], in_=banks[bank][:].rearrange("p c r j -> p r j c")
            )

        strip_stats = keep.tile([P, HALVES, STRIPS, 6], F32)

        def strip_moments(hr):
            for e in range(STRIPS):
                cols = slice(SHIFT + e * SHIFT, SHIFT + (e + 1) * SHIFT)
                nc.vector.bn_stats(
                    out=strip_stats[:, hr, e, :],
                    in_=detail[:, hr * HALF_ROWS : (hr + 1) * HALF_ROWS, cols, :].rearrange("p r l c -> p r (l c)"),
                )

        def send_below():
            for i in range(GRID - 1):
                nc.sync.dma_start(out=below[i:P:GRID, :, :, :], in_=detail[i + 1 : P : GRID, 0:HALF_ROWS, :, :])

        def send_above():
            for i in range(GRID - 1):
                nc.sync.dma_start(out=above[i + 1 : P : GRID, :, :, :], in_=detail[i:P:GRID, HALF_ROWS:PATCH, :, :])

        warm = acc_psum.tile([P, P], F32, tag="wide1")

        def keep_clock(columns):
            nc.tensor.matmul(out=warm[:, 0:columns], lhsT=ident[:], rhs=ident[:, 0:columns], start=True, stop=True)

        keep_clock(P)
        keep_clock(P)
        for c in range(CH):
            haar_taps(1, c)
            if c < CH - 1:
                keep_clock(P // 2)
        haar_vector()
        haar_join(1)
        send_below()
        load_w(1)
        for c in range(CH):
            for bank in (2, 3):
                haar_taps(bank, c)
        haar_copy(2)
        haar_copy(3)
        regroup_w("scalar", 0, REST)
        strip_moments(0)
        send_above()
        load_w(2)
        load_w(3)
        for m in range(4):
            load_tok(m)
        load_w(4)
        strip_moments(1)
        rows_f32 = keep.tile([P, PACK + 1, P], F32)
        nc.scalar.copy(
            out=rows_f32[:, 0:PACK, :].rearrange("p t (a e) -> p a t e", e=4),
            in_=rows_in[:, 0:PASS_K].rearrange("p (a t e) -> p a t e", t=PACK, e=4),
        )
        nc.scalar.copy(out=rows_f32[:, PACK, :], in_=rows_in[:, PASS_K:])
        gain_ps = acc_psum.tile([P, PACK, P], F32, tag="wide0")
        b2_ps = acc_psum.tile([P, P], F32, tag="rest0")
        for t in range(PACK):
            nc.tensor.transpose(out=gain_ps[:, t, :], in_=rows_f32[:, t, :], identity=ident[:])
        nc.tensor.transpose(out=b2_ps[:], in_=rows_f32[:, PACK, :], identity=ident[:])
        regroup_w("scalar", 0, slice(N_WIDE // 2, N_WIDE))
        gain_t = keep.tile([P, PACK, P], F32)
        b2_t = keep.tile([P, DIM // P], F32)
        nc.scalar.copy(out=b2_t[:], in_=b2_ps[:, 0 : DIM // P])
        nc.scalar.copy(out=gain_t[:], in_=gain_ps[:])
        b2_all = keep.tile([P, DIM], BF16)

        def add_bias(m):
            nc.vector.tensor_tensor(out=tok_bias[:, m, :], in0=tok_in[:, m, :], in1=b2_all[:], op=ALU.add)


        def fill(n):
            g, first = (0, 0) if n < 4 else (1, 4)
            regroup_w("vector", g, slice(64 * (n - first), 64 * (n - first + 1)))


        means = strip_stats[:].rearrange("p h e (o f) -> p h e o f", o=2)[:, :, :, :, 1]
        spreads = strip_stats[:].rearrange("p h e (o f) -> p h e o f", o=2)[:, :, :, :, 2]
        mean_squares = keep.tile([P, HALVES, STRIPS, 2], F32)
        nc.vector.tensor_tensor(out=mean_squares[:], in0=means, in1=means, op=ALU.mult)
        nc.vector.tensor_copy(out=sums[:, :, 0, 1 : 1 + STRIPS, :], in_=means)
        fill(0)
        nc.vector.scalar_tensor_tensor(
            out=sums[:, :, 1, 1 : 1 + STRIPS, :].rearrange("p h e o -> p h (e o)"),
            in0=mean_squares[:].rearrange("p h e o -> p (h e o)"),
            scalar=float(STRIP_HALF),
            in1=strip_stats[:].rearrange("p h e (o f) -> p (h e o) f", o=2)[:, :, 2],
            op0=ALU.mult,
            op1=ALU.add,
        )
        fill(1)
        inner = keep.tile([P, HALVES * 2, GRID], F32)
        across = keep.tile([P, HALVES * 2, GRID + 1], F32)
        outer = keep.tile([P, HALVES * 2, GRID], F32)
        both = keep.tile([P, HALVES * 2, GRID], F32)
        own = keep.tile([P, 2, GRID], F32)
        nc.vector.tensor_reduce(
            out=across[:], in_=sums[:].rearrange("p h q (j v) o -> p (h q) j (v o)", v=2), axis=AX.X, op=ALU.add
        )
        nc.vector.tensor_reduce(
            out=inner[:],
            in_=sums[:, :, :, 1 : 1 + STRIPS, :].rearrange("p h q (j v) o -> p (h q) j (v o)", v=2),
            axis=AX.X,
            op=ALU.add,
        )
        nc.vector.tensor_tensor(out=outer[:], in0=across[:, :, 0:GRID], in1=across[:, :, 1 : GRID + 1], op=ALU.add)
        fill(2)
        nc.vector.tensor_tensor(out=both[:], in0=outer[:], in1=inner[:], op=ALU.add)
        fill(3)
        nc.vector.tensor_tensor(out=own[:], in0=both[:, 0:2, :], in1=both[:, 2:4, :], op=ALU.add)
        moments = turn_psum.tile([P, 2, GRID], F32, tag="turned")
        terms = ((sum_above, outer[:, 2:4, :]), (sum_below, outer[:, 0:2, :]), (sum_own, own[:]))
        for n, (mat, part_sums) in enumerate(terms):
            nc.tensor.matmul(
                out=moments[:].rearrange("p q j -> p (q j)"),
                lhsT=mat[:],
                rhs=part_sums.rearrange("p q j -> p (q j)"),
                start=(n == 0),
                stop=(n == len(terms) - 1),
            )
        b2_wide = acc_psum.tile([P, N_WIDE], F32, tag="wide1")
        b2_rest = acc_psum.tile([P, DIM - N_WIDE], F32, tag="rest1")
        for s in range(DIM // P):
            bank, first = (b2_wide, 0) if s < N_WIDE // P else (b2_rest, N_WIDE // P)
            nc.tensor.transpose(
                out=bank[:, (s - first) * P : (s - first + 1) * P],
                in_=b2_t[:, s : s + 1].to_broadcast([P, P]),
                identity=ident[:],
            )
        quantise_w(0)
        mean = keep.tile([P, GRID], F32)
        mean_sq = keep.tile([P, GRID], F32)
        var = keep.tile([P, GRID], F32)
        std = keep.tile([P, GRID], F32)
        rstd = keep.tile([P, GRID], F32)
        shift = keep.tile([P, GRID], F32)
        nc.scalar.activation(out=mean_sq[:], in_=moments[:, 0, :], func=ACT.Square, scale=float(STRIP_HALF))
        nc.vector.tensor_scalar(out=mean[:], in0=moments[:, 0, :], scalar1=float(STRIP_HALF), scalar2=None, op0=ALU.mult)
        nc.vector.scalar_tensor_tensor(
            out=var[:], in0=moments[:, 1, :], scalar=EPS, in1=mean_sq[:], op0=ALU.add, op1=ALU.subtract
        )
        nc.scalar.activation(out=std[:], in_=var[:], func=ACT.Sqrt)
        nc.scalar.copy(out=b2_all[:, WIDE], in_=b2_wide[:])
        fill(4)
        fill(5)
        nc.vector.reciprocal(out=rstd[:], in_=std[:])
        nc.vector.scalar_tensor_tensor(out=shift[:], in0=mean[:], scalar=-1.0, in1=rstd[:], op0=ALU.mult, op1=ALU.mult)

        def normalise(engine, j, s, parts=(0, 1)):
            first = SHIFT + PATCH * j + (0, -SHIFT, SHIFT, -SHIFT, SHIFT)[s]
            if s == 0:
                pieces = ((detail, 0, 0, PATCH),)
            elif s in (1, 2):
                pieces = ((detail, 0, HALF_ROWS, HALF_ROWS), (above, 0, 0, HALF_ROWS))
            else:
                pieces = ((detail, HALF_ROWS, 0, HALF_ROWS), (below, 0, HALF_ROWS, HALF_ROWS))
            base = 2 * PLANE_PITCH * j
            if s % 2 == 0:
                start, step = base + UNIT * (s // 2), PLANE_PITCH + 2 * UNIT
            else:
                start, step = base + UNIT * (s // 2 + 3), PLANE_PITCH - 3 * UNIT
            target = normed[:, start : start + 2 * step].rearrange("p (l f) -> p l f", l=2)[:, :, 0:PLANE_LEN]
            target = target.rearrange("p l (r h u) -> p r h l u", r=PATCH, u=PAIR)[:, :, :, :, 0:UNIT]
            if s % 2 == 1:
                target = target[:, :, :, ::-1, :]
            for part in parts if s > 0 else (0,):
                tile, row, to_row, count = pieces[part]
                source = tile[:, row : row + count, first : first + PATCH, :].rearrange("p r (h l) c -> p r h l c", l=2)
                goal = target[:, to_row : to_row + count, :, :, :]
                if engine == "scalar":
                    nc.scalar.activation(
                        out=goal, in_=source, func=ACT.Identity, scale=rstd[:, j : j + 1], bias=shift[:, j : j + 1]
                    )
                else:
                    nc.vector.tensor_scalar(
                        out=goal,
                        in0=source,
                        scalar1=mean[:, j : j + 1],
                        scalar2=rstd[:, j : j + 1],
                        op0=ALU.subtract,
                        op1=ALU.mult,
                    )

        turned_tiles = {}

        def turn(grp, g):
            columns = [J_TILE * m + j for m in TILE_GROUPS[grp] for j in range(J_TILE)]
            pairs = [(parity, j) for parity in range(2) for j in columns]
            for first in range(0, len(pairs), 4):
                turned = turn_psum.tile([P, 4, P], F32)
                turned_tiles[(grp, g, first // 4)] = turned
                for n, (parity, j) in enumerate(pairs[first : first + 4]):
                    at = PLANE_PITCH * (2 * j + parity) + P * g
                    nc.tensor.transpose(out=turned[:, n, :], in_=normed[:, at : at + P], identity=turn_order[:])

        def tokens(grp):
            tiles = TILE_GROUPS[grp]
            return slice(TILE_TOKENS * tiles[0], TILE_TOKENS * (tiles[-1] + 1))

        def empty(grp, g):
            count = len(TILE_GROUPS[grp])
            for parity in range(2):
                bank, first = divmod(parity * count * J_TILE, 4)
                turned = turned_tiles[(grp, g, bank)][:, first : first + count * J_TILE, :]
                turned = turned.rearrange("p (m j) (h r) -> p h m r j", j=J_TILE, h=CH_HALVES)
                for h in range(CH_HALVES):
                    t = 2 * parity + h
                    nc.scalar.activation(
                        out=planes[:, g, t, tokens(grp)].rearrange("p (m r j) -> p m r j", m=count, j=J_TILE),
                        in_=turned[:, h, :, :, :],
                        func=ACT.Identity,
                        scale=gain_t[:, t, g : g + 1],
                        bias=gain_t[:, t, 32 + g : 33 + g],
                    )

        z_grps = {}

        def regroup_z(grp, g, engine="vector"):
            count = len(TILE_GROUPS[grp]) * TILE_TOKENS
            z_grp = z_grp_pool.tile([P, 2 * TILE_TOKENS, PACK], BF16, align_bytes=64)
            z_grps[(grp, g)] = z_grp
            grouped = z_grp[:, 0:count, :].rearrange("p (w i) t -> p w t i", i=4)
            rows = planes[:, g, :, tokens(grp)].rearrange("p t (w i) -> p w t i", i=4)
            if engine == "scalar":
                nc.scalar.copy(out=grouped, in_=rows)
            else:
                nc.vector.tensor_copy(out=grouped, in_=rows)

        def quantise_z(grp, g):
            count = len(TILE_GROUPS[grp]) * TILE_TOKENS
            nc.vector.quantize_mx(
                out=z_codes[:, g, tokens(grp)].bitcast(FP8X4),
                scales=z_scales[:, g, tokens(grp)],
                in_=z_grps[(grp, g)][:, 0:count, :].rearrange("p w t -> p (w t)"),
            )

        accs = {}

        def multiply(grp, g):
            for m in TILE_GROUPS[grp]:
                rows = slice(m * P, (m + 1) * P)
                if g == 0:
                    acc_wide = acc_psum.tile([P, N_WIDE], F32, tag="wide%d" % (m % 2))
                    acc_rest = acc_psum.tile([P, DIM - N_WIDE], F32, tag="rest%d" % (m % 2))
                    accs[m] = ((acc_wide, WIDE), (acc_rest, REST))
                for acc, cols in accs[m]:
                    nc.tensor.matmul_mx(
                        out=acc[:],
                        lhsT=z_codes[:, g, rows].bitcast(FP8X4),
                        lhsT_scale=z_scales[:, g, rows],
                        rhs=w_codes[:, g, cols].bitcast(FP8X4),
                        rhs_scale=w_scales[:, g, cols],
                        start=(g == 0),
                        stop=(g == PASSES - 1),
                    )

        def finish(m):
            for acc, cols in accs[m]:
                nc.vector.tensor_tensor(out=tok_bias[:, m, cols], in0=acc[:], in1=tok_bias[:, m, cols], op=ALU.add)
                nc.sync.dma_start(out=token_rows(out, m)[:, :, cols], in_=tok_bias[:, m, cols])

        def normalise_columns(engine, columns):
            for kind in ((0, 2, 4), (1, 3)):
                for j in columns:
                    for s in kind:
                        for part in range(2 if s > 0 else 1):
                            normalise(engine, j, s, (part,))

        steps = [(grp, g) for grp in range(len(TILE_GROUPS)) for g in range(PASSES)]
        normalise_columns("scalar", (3,))
        nc.scalar.copy(out=b2_all[:, REST], in_=b2_rest[:])
        regroup_w("scalar", 1, REST)
        normalise_columns("vector", (0, 1, 2,))
        regroup_w("vector", 1, slice(128, N_WIDE))
        quantise_w(1)
        multiply_after = {2: [0], 3: [1], 4: [2], 5: [3], 6: [4], 7: [5, 6], 8: [7], 9: [8, 9]}
        turn(*steps[0])
        turn(*steps[1])
        for n in range(len(steps)):
            empty(*steps[n])
            regroup_z(*steps[n], "scalar" if n in (3, 6, 9) else "vector")
            if n == 0:
                normalise_columns("vector", (4, 5,))
            if n == 1:
                normalise_columns("scalar", (7,))
                normalise_columns("vector", (6,))
                regroup_w("vector", 2, WIDE)
                regroup_w("scalar", 2, REST)
            if n == 2:
                quantise_w(2)
                regroup_w("vector", 3, WIDE)
                regroup_w("scalar", 3, REST)
            if n == 3:
                quantise_w(3)
                add_bias(0)
            if n == 4:
                regroup_w("vector", 4, WIDE)
                regroup_w("scalar", 4, REST)
                add_bias(1)
            if n == 5:
                quantise_w(4)
            if n == 6:
                add_bias(2)
            if n == 7:
                finish(0)
                finish(1)
            quantise_z(*steps[n])
            if n + 2 < len(steps):
                turn(*steps[n + 2])
            for done in multiply_after.get(n, []):
                multiply(*steps[done])
        add_bias(3)
        finish(2)
        finish(3)
